import numpy as np
import ml_dtypes


def mxq(x, axis, fmt="e4m3"):
    dtype, down = {"e4m3": (ml_dtypes.float8_e4m3fn, 7), "e5m2": (ml_dtypes.float8_e5m2, 14)}[fmt]
    v = np.moveaxis(np.asarray(x, np.float32).astype(ml_dtypes.bfloat16).astype(np.float64), axis, -1)
    blocks = v.reshape(v.shape[:-1] + (-1, 32))
    amax = np.abs(blocks).max(-1, keepdims=True)
    byte = np.maximum(np.where(amax > 0, np.frexp(amax)[1] - 1 + 127, 0) - down, 1)
    scale = np.exp2(byte - 127.0)
    codes = (blocks / scale).astype(np.float32).astype(dtype).astype(np.float64)
    return np.moveaxis((codes * scale).reshape(v.shape), -1, axis)


WIDE = False


def mx_kscale(k):
    if not WIDE:
        return np.ones(k)
    levels = np.array([10, -10, 5, -5, 0])
    a = np.random.permutation(np.resize(levels, k // 512 * 4)).reshape(k // 512, 4)
    idx = np.arange(k)
    return np.exp2(a[idx // 512, idx % 128 // 32])


BF16 = ml_dtypes.bfloat16


def bf(x):
    return np.asarray(x, np.float32).astype(BF16)


def f64(x):
    return np.asarray(x).astype(np.float64)


B, L, D, R = 8, 1024, 512, 256


def setup_inputs():
    s = mx_kscale(D)
    t = np.exp2(np.round(np.log2(mx_kscale(D)) / 2))
    return {"query": bf(np.random.standard_normal((B, L, D)) * s),
            "Wq": bf(np.random.standard_normal((D, D)) / np.sqrt(D) * t[:, None] / s[None, :]),
            "bq": bf(np.random.standard_normal(D) * 0.3 * t),
            "centers": bf(np.random.random((R, D)) * t),
            "widths": bf(np.random.uniform(0.1, 1.0, (R, D)) * t)}


def reference(query, Wq, bq, centers, widths):
    q = (mxq(f64(query), 2, "e4m3") @ mxq(f64(Wq), 1, "e4m3").T) + f64(bq)
    c, w = f64(centers), f64(widths)
    inv_w2 = 1.0 / (w * w)
    qq = mxq(q * q, 2, "e4m3") @ mxq(inv_w2, 1, "e4m3").T
    qc = mxq(q, 2, "e4m3") @ mxq(c * inv_w2, 1, "e4m3").T
    cc = np.sum(c * c * inv_w2, axis=-1)
    return -(0.5 / D) * (qq - 2.0 * qc + cc)

@@ -1,0 +1,297 @@
+from contextlib import ExitStack
+
+import concourse.bass as bass
+import concourse.mybir as mybir
+import concourse.tile as tile
+from concourse.masks import make_identity
+
+F32 = mybir.dt.float32
+BF16 = mybir.dt.bfloat16
+U32 = mybir.dt.uint32
+U8 = mybir.dt.uint8
+FP8X4 = mybir.dt.float8_e4m3fn_x4
+ALU = mybir.AluOpType
+ACT = mybir.ActivationFunctionType
+
+P = 128
+TOKENS = 8192
+D = 512
+R = 256
+NQUAD = TOKENS // 512
+NPAIR = TOKENS // 256
+SCALE = -(0.5 / D)
+FLOPS = 2 * TOKENS * D * D + 2 * 2 * TOKENS * D * R
+
+LEAD_T = 4
+LEAD_Q = 3
+LAG_QQ = 2
+LAG_M2 = 3
+FIRST_M2_STEP = 4
+CAST_SPLIT = 896
+TAIL_PAIRS = 2
+
+
+def tile_fuzzy_attention_pa_t_kernel(tc, query, Wq, bq, centers, widths, out):
+    nc = tc.nc
+    xv = query.flatten_outer_dims().rearrange("(j p a) i -> j p a i", p=P, a=4)
+    ov = out.flatten_outer_dims().rearrange("(j p a) r -> j p a r", p=P, a=4)
+
+    with ExitStack() as ctx:
+        ctx.enter_context(tc.manual_schedule())
+        const = ctx.enter_context(tc.tile_pool(name="const", bufs=1))
+        ring = ctx.enter_context(tc.tile_pool(name="ring", bufs=4))
+        psum = ctx.enter_context(tc.psum_pool(name="psum", bufs=2))
+
+        x_sb = [const.tile([P, 4, D], BF16, name="x%d" % j) for j in range(NQUAD)]
+        wq_sb = const.tile([P, 4, D], BF16, name="wq_sb")
+        bq_sb = const.tile([P, 4], BF16, name="bq_sb")
+        w_sb = const.tile([P, 2, D], BF16, name="w_sb")
+        c_sb = const.tile([P, 2, D], BF16, name="c_sb")
+        nc.sync.dma_start(out=x_sb[0][:, 0:2, :], in_=xv[0][:, 0:2, :])
+        nc.sync.dma_start(out=wq_sb[:], in_=Wq.rearrange("(c m) i -> c m i", m=4))
+        nc.sync.dma_start(out=bq_sb[:], in_=bq.rearrange("(c m) -> c m", m=4))
+        nc.sync.dma_start(out=x_sb[0][:, 2:4, :], in_=xv[0][:, 2:4, :])
+        nc.sync.dma_start(out=w_sb[:], in_=widths.rearrange("(t p) d -> p t d", p=P))
+        nc.sync.dma_start(out=c_sb[:], in_=centers.rearrange("(t p) d -> p t d", p=P))
+        for j in range(1, NQUAD):
+            nc.sync.dma_start(out=x_sb[j][:], in_=xv[j])
+
+        ident = const.tile([P, P], F32, name="ident")
+        make_identity(nc, ident[:])
+        bias = const.tile([P, 4], F32, name="bias")
+        nc.vector.tensor_copy(out=bias[:], in_=bq_sb[:])
+
+        wg = const.tile([P, 2048], BF16, name="wg", align_bytes=64)
+        wc = const.tile([P, 512], U32, name="wc", align_bytes=64)
+        ws = const.tile([P, 512], U8, name="ws", align_bytes=64)
+        w2 = const.tile([P, 2, 4, P], F32, name="w2")
+        iw = const.tile([P, 2, 4, P], F32, name="iw")
+        ciw = const.tile([P, 2, 4, P], F32, name="ciw")
+        t1 = const.tile([P, 2, 4, P], F32, name="t1")
+        cc = const.tile([P, 2], F32, name="cc")
+        ccs = const.tile([P, R], F32, name="ccs")
+        rg = const.tile([P, 2, R, 4], BF16, name="rg", align_bytes=64)
+        rc = const.tile([P, 512], U32, name="rc", align_bytes=64)
+        rs = const.tile([P, 512], U8, name="rs", align_bytes=64)
+        zs = [const.tile([P, 4, R], F32, name="zs%d" % j) for j in range(NQUAD)]
+
+        tb = {}
+        xg = {}
+        xc = {}
+        xs = {}
+        ab = {}
+        qf = {}
+        gq = {}
+        qc = {}
+        qs = {}
+        zb = {}
+        rtb = {}
+
+        def st_t(j):
+            tb[j] = psum.tile([P, 2, 2, P], F32, name="tb%d" % j, tag="T", bufs=2)
+            for a in range(2):
+                words = x_sb[j // 2][:, 2 * (j % 2) + a, :].bitcast(F32)
+                for u in range(2):
+                    nc.tensor.transpose(tb[j][:, a, u, :], words[:, u * P:(u + 1) * P], ident[:])
+
+        def st_x(j):
+            xg[j] = ring.tile([P, 1024], BF16, name="xg%d" % j, tag="xg", bufs=3, align_bytes=64)
+            nc.scalar.copy(
+                out=xg[j][:].bitcast(F32).rearrange("p (a t u) -> p a t u", a=2, u=2),
+                in_=tb[j][:].rearrange("p a u t -> p a t u"),
+            )
+
+        def st_qx(j):
+            xc[j] = ring.tile([P, 256], U32, name="xc%d" % j, tag="xc", bufs=4, align_bytes=64)
+            xs[j] = ring.tile([P, 256], U8, name="xs%d" % j, tag="xs", bufs=4, align_bytes=64)
+            nc.vector.quantize_mx(out=xc[j][:].bitcast(FP8X4), scales=xs[j][:], in_=xg[j][:])
+
+        def st_m1(j):
+            for a in range(2):
+                acc = psum.tile([P, 4, P], F32, name="ab%d_%d" % (j, a), tag="A", bufs=4)
+                ab[(j, a)] = acc
+                for m in range(4):
+                    nc.tensor.matmul_mx(
+                        out=acc[:, m, :],
+                        lhsT=wc[:, m * P:(m + 1) * P].bitcast(FP8X4),
+                        lhsT_scale=ws[:, m * P:(m + 1) * P],
+                        rhs=xc[j][:, a * P:(a + 1) * P].bitcast(FP8X4),
+                        rhs_scale=xs[j][:, a * P:(a + 1) * P],
+                        start=True,
+                        stop=True,
+                    )
+
+        def st_p(j):
+            qf[j] = ring.tile([P, 2, P, 4], F32, name="qf%d" % j, tag="qf", bufs=3)
+            for a in range(2):
+                nc.vector.tensor_tensor(
+                    out=qf[j][:, a, :, :],
+                    in0=ab[(j, a)][:].rearrange("p m t -> p t m"),
+                    in1=bias[:].unsqueeze(1).to_broadcast([P, P, 4]),
+                    op=ALU.add,
+                )
+
+        def split(j):
+            return 0 if j >= NPAIR - TAIL_PAIRS else CAST_SPLIT
+
+        def get_gq(j):
+            if j not in gq:
+                gq[j] = ring.tile([P, 2, 1024], BF16, name="gq%d" % j, tag="gq", bufs=4, align_bytes=64)
+            return gq[j]
+
+        def st_cv(j):
+            s = split(j)
+            flat = qf[j][:].rearrange("p a t m -> p (a t m)")
+            nc.vector.tensor_copy(out=get_gq(j)[:, 1, s:1024], in_=flat[:, s:1024])
+
+        def st_sq(j):
+            s = split(j)
+            flat = qf[j][:].rearrange("p a t m -> p (a t m)")
+            nc.scalar.activation(out=get_gq(j)[:, 0, :], in_=flat, func=ACT.Square)
+            if s > 0:
+                nc.scalar.copy(out=get_gq(j)[:, 1, 0:s], in_=flat[:, 0:s])
+
+        def st_qq(j):
+            qc[j] = ring.tile([P, 512], U32, name="qc%d" % j, tag="qc", bufs=4, align_bytes=64)
+            qs[j] = ring.tile([P, 512], U8, name="qs%d" % j, tag="qs", bufs=4, align_bytes=64)
+            nc.vector.quantize_mx(
+                out=qc[j][:].bitcast(FP8X4),
+                scales=qs[j][:],
+                in_=gq[j][:].rearrange("p k c -> p (k c)"),
+            )
+
+        def st_m2(j):
+            zb[j] = psum.tile([P, 2, R], F32, name="zb%d" % j, tag="Z", bufs=2)
+            for a in range(2):
+                for k in range(2):
+                    lo = k * 256 + a * P
+                    nc.tensor.matmul_mx(
+                        out=zb[j][:, a, :],
+                        lhsT=qc[j][:, lo:lo + P].bitcast(FP8X4),
+                        lhsT_scale=qs[j][:, lo:lo + P],
+                        rhs=rc[:, k * R:(k + 1) * R].bitcast(FP8X4),
+                        rhs_scale=rs[:, k * R:(k + 1) * R],
+                        start=(k == 0),
+                        stop=(k == 1),
+                    )
+
+        def st_z(j):
+            h = 2 * (j % 2)
+            nc.vector.scalar_tensor_tensor(
+                out=zs[j // 2][:, h:h + 2, :],
+                in0=zb[j][:],
+                scalar=SCALE,
+                in1=ccs[:].unsqueeze(1).to_broadcast([P, 2, R]),
+                op0=ALU.mult,
+                op1=ALU.add,
+            )
+            if j >= NPAIR - 2:
+                nc.sync.dma_start(out=ov[j // 2][:, h:h + 2, :], in_=zs[j // 2][:, h:h + 2, :])
+            elif j % 2 == 1:
+                nc.sync.dma_start(out=ov[j // 2], in_=zs[j // 2][:])
+
+        def perm(t):
+            return t[:].rearrange("p t (c m) -> p t m c", m=4)
+
+        def st_rt(k):
+            src = iw if k < 2 else ciw
+            rtb[k] = psum.tile([P, 4, P], F32, name="rtb%d" % k, tag="Z", bufs=2)
+            for m in range(4):
+                nc.tensor.transpose(rtb[k][:, m, :], src[:, k % 2, m, :], ident[:])
+
+        def st_rx(k):
+            nc.scalar.activation(
+                out=rg[:, k // 2, (k % 2) * P:(k % 2 + 1) * P, :],
+                in_=rtb[k][:].rearrange("p m r -> p r m"),
+                func=ACT.Copy,
+                scale=(1.0 if k < 2 else -2.0),
+            )
+
+        st_t(0)
+        st_x(0)
+        twb = []
+        for h in range(2):
+            t = psum.tile([P, 2, 2, P], F32, name="twb%d" % h, tag="A", bufs=4)
+            twb.append(t)
+            for m in range(2):
+                words = wq_sb[:, 2 * h + m, :].bitcast(F32)
+                for u in range(2):
+                    nc.tensor.transpose(t[:, m, u, :], words[:, u * P:(u + 1) * P], ident[:])
+        wgv = wg[:].bitcast(F32).rearrange("p (m c u) -> p m c u", m=4, u=2)
+        nc.scalar.copy(out=wgv[:, 0:2], in_=twb[0][:].rearrange("p m u c -> p m c u"))
+        nc.vector.tensor_copy(out=wgv[:, 2:4], in_=twb[1][:].rearrange("p m u c -> p m c u"))
+        st_qx(0)
+        nc.vector.quantize_mx(out=wc[:].bitcast(FP8X4), scales=ws[:], in_=wg[:])
+        st_t(1)
+        st_x(1)
+        st_qx(1)
+        st_m1(0)
+        nc.scalar.activation(out=w2[:], in_=perm(w_sb), func=ACT.Square)
+        for j in range(2, LEAD_T):
+            st_t(j)
+            st_x(j)
+        for j in range(2, LEAD_Q):
+            st_qx(j)
+
+        m2_at = {}
+        for j in range(NPAIR):
+            s = max(j + LAG_M2, FIRST_M2_STEP)
+            m2_at[s] = m2_at.get(s, []) + [j]
+
+        for s in range(NPAIR + LAG_M2 + 1):
+            if s + LEAD_T < NPAIR:
+                st_t(s + LEAD_T)
+            if s == 1:
+                st_rt(0)
+                st_rt(1)
+            if s == 2:
+                st_rt(2)
+                st_rt(3)
+            if s == 4:
+                ccp = psum.tile([P, R], F32, name="ccp", tag="Z", bufs=2)
+                for t in range(2):
+                    nc.tensor.matmul(
+                        out=ccp[:, t * P:(t + 1) * P],
+                        lhsT=cc[:, t:t + 1].to_broadcast([P, P]),
+                        rhs=ident[:],
+                        start=True,
+                        stop=True,
+                    )
+                nc.scalar.activation(out=ccs[:], in_=ccp[:], func=ACT.Copy, scale=SCALE)
+            for j in m2_at.get(s, []):
+                st_m2(j)
+            if s + 1 < NPAIR:
+                st_m1(s + 1)
+            if s < NPAIR:
+                st_p(s)
+            if s == 0:
+                nc.vector.reciprocal(out=iw[:], in_=w2[:])
+                nc.gpsimd.tensor_tensor(out=ciw[:], in0=perm(c_sb), in1=iw[:], op=ALU.mult)
+                nc.gpsimd.tensor_tensor(out=t1[:], in0=perm(c_sb), in1=ciw[:], op=ALU.mult)
+            if 0 <= s - LAG_QQ < NPAIR:
+                st_qq(s - LAG_QQ)
+            if s < NPAIR:
+                st_cv(s)
+            for j in m2_at.get(s, []):
+                st_z(j)
+            if s + LEAD_Q < NPAIR:
+                st_qx(s + LEAD_Q)
+            if s == 3:
+                nc.vector.quantize_mx(
+                    out=rc[:].bitcast(FP8X4), scales=rs[:], in_=rg[:].rearrange("p k r m -> p (k r m)")
+                )
+            if s < NPAIR:
+                st_sq(s)
+            if s == 1:
+                st_rx(0)
+                st_rx(1)
+            if s == 2:
+                st_rx(2)
+                st_rx(3)
+            if s == 3:
+                for t in range(2):
+                    nc.scalar.activation(
+                        out=t1[:, t], in_=t1[:, t], func=ACT.Copy, accum_out=cc[:, t:t + 1]
+                    )
+            if s + LEAD_T < NPAIR:
+                st_x(s + LEAD_T)

@@ -1,8 +1,6 @@
 from contextlib import ExitStack
 
-import concourse.bass as bass
 import concourse.mybir as mybir
-import concourse.tile as tile
 from concourse.masks import make_identity
 
 F32 = mybir.dt.float32
@@ -22,13 +20,22 @@ NPAIR = TOKENS // 256
 SCALE = -(0.5 / D)
 FLOPS = 2 * TOKENS * D * D + 2 * 2 * TOKENS * D * R
 
-LEAD_T = 4
-LEAD_Q = 3
-LAG_QQ = 2
-LAG_M2 = 3
-FIRST_M2_STEP = 4
-CAST_SPLIT = 896
-TAIL_PAIRS = 2
+S_FIRST = 3
+S_LAST = 29
+G_FIRST = 2
+G_LAST = 29
+
+
+def s_tile(j):
+    return j % 2 == 1 and S_FIRST <= j <= S_LAST
+
+
+def caster(j):
+    if j < G_FIRST:
+        return "S"
+    if j > G_LAST:
+        return "V"
+    return "G"
 
 
 def tile_fuzzy_attention_pa_t_kernel(tc, query, Wq, bq, centers, widths, out):
@@ -50,9 +57,9 @@ def tile_fuzzy_attention_pa_t_kernel(tc, query, Wq, bq, centers, widths, out):
         nc.sync.dma_start(out=x_sb[0][:, 0:2, :], in_=xv[0][:, 0:2, :])
         nc.sync.dma_start(out=wq_sb[:], in_=Wq.rearrange("(c m) i -> c m i", m=4))
         nc.sync.dma_start(out=bq_sb[:], in_=bq.rearrange("(c m) -> c m", m=4))
-        nc.sync.dma_start(out=x_sb[0][:, 2:4, :], in_=xv[0][:, 2:4, :])
         nc.sync.dma_start(out=w_sb[:], in_=widths.rearrange("(t p) d -> p t d", p=P))
         nc.sync.dma_start(out=c_sb[:], in_=centers.rearrange("(t p) d -> p t d", p=P))
+        nc.sync.dma_start(out=x_sb[0][:, 2:4, :], in_=xv[0][:, 2:4, :])
         for j in range(1, NQUAD):
             nc.sync.dma_start(out=x_sb[j][:], in_=xv[j])
 
@@ -81,13 +88,19 @@ def tile_fuzzy_attention_pa_t_kernel(tc, query, Wq, bq, centers, widths, out):
         xs = {}
         ab = {}
         qf = {}
+        qfp = {}
         gq = {}
         qc = {}
         qs = {}
         zb = {}
         rtb = {}
 
+        def ok(j):
+            return 0 <= j < NPAIR
+
         def st_t(j):
+            if not ok(j):
+                return
             tb[j] = psum.tile([P, 2, 2, P], F32, name="tb%d" % j, tag="T", bufs=2)
             for a in range(2):
                 words = x_sb[j // 2][:, 2 * (j % 2) + a, :].bitcast(F32)
@@ -95,6 +108,8 @@ def tile_fuzzy_attention_pa_t_kernel(tc, query, Wq, bq, centers, widths, out):
                     nc.tensor.transpose(tb[j][:, a, u, :], words[:, u * P:(u + 1) * P], ident[:])
 
         def st_x(j):
+            if not ok(j):
+                return
             xg[j] = ring.tile([P, 1024], BF16, name="xg%d" % j, tag="xg", bufs=3, align_bytes=64)
             nc.scalar.copy(
                 out=xg[j][:].bitcast(F32).rearrange("p (a t u) -> p a t u", a=2, u=2),
@@ -102,11 +117,15 @@ def tile_fuzzy_attention_pa_t_kernel(tc, query, Wq, bq, centers, widths, out):
             )
 
         def st_qx(j):
+            if not ok(j):
+                return
             xc[j] = ring.tile([P, 256], U32, name="xc%d" % j, tag="xc", bufs=4, align_bytes=64)
             xs[j] = ring.tile([P, 256], U8, name="xs%d" % j, tag="xs", bufs=4, align_bytes=64)
             nc.vector.quantize_mx(out=xc[j][:].bitcast(FP8X4), scales=xs[j][:], in_=xg[j][:])
 
         def st_m1(j):
+            if not ok(j):
+                return
             for a in range(2):
                 acc = psum.tile([P, 4, P], F32, name="ab%d_%d" % (j, a), tag="A", bufs=4)
                 ab[(j, a)] = acc
@@ -121,9 +140,14 @@ def tile_fuzzy_attention_pa_t_kernel(tc, query, Wq, bq, centers, widths, out):
                         stop=True,
                     )
 
-        def st_p(j):
-            qf[j] = ring.tile([P, 2, P, 4], F32, name="qf%d" % j, tag="qf", bufs=3)
-            for a in range(2):
+        def first_v(j):
+            return 1 if s_tile(j) else 0
+
+        def st_pv(j):
+            if not ok(j):
+                return
+            qf[j] = ring.tile([P, 2, P, 4], F32, name="qf%d" % j, tag="qf", bufs=4)
+            for a in range(first_v(j), 2):
                 nc.vector.tensor_tensor(
                     out=qf[j][:, a, :, :],
                     in0=ab[(j, a)][:].rearrange("p m t -> p t m"),
@@ -131,27 +155,54 @@ def tile_fuzzy_attention_pa_t_kernel(tc, query, Wq, bq, centers, widths, out):
                     op=ALU.add,
                 )
 
-        def split(j):
-            return 0 if j >= NPAIR - TAIL_PAIRS else CAST_SPLIT
+        def st_ps(j):
+            if not ok(j) or not s_tile(j):
+                return
+            qfp[j] = ring.tile([P, 4, P], F32, name="qfp%d" % j, tag="qfp", bufs=2)
+            for m in range(4):
+                nc.scalar.activation(
+                    out=qfp[j][:, m, :], in_=ab[(j, 0)][:, m, :], func=ACT.Identity, bias=bias[:, m:m + 1]
+                )
 
         def get_gq(j):
             if j not in gq:
                 gq[j] = ring.tile([P, 2, 1024], BF16, name="gq%d" % j, tag="gq", bufs=4, align_bytes=64)
             return gq[j]
 
-        def st_cv(j):
-            s = split(j)
-            flat = qf[j][:].rearrange("p a t m -> p (a t m)")
-            nc.vector.tensor_copy(out=get_gq(j)[:, 1, s:1024], in_=flat[:, s:1024])
+        def st_sqs(j):
+            if not ok(j) or not s_tile(j):
+                return
+            src = qfp[j][:].rearrange("p m t -> p t m")
+            nc.scalar.activation(
+                out=get_gq(j)[:, 0, 0:512].rearrange("p (t m) -> p t m", m=4), in_=src, func=ACT.Square
+            )
+            nc.scalar.copy(out=get_gq(j)[:, 1, 0:512].rearrange("p (t m) -> p t m", m=4), in_=src)
 
         def st_sq(j):
-            s = split(j)
+            if not ok(j):
+                return
+            lo = 512 * first_v(j)
             flat = qf[j][:].rearrange("p a t m -> p (a t m)")
-            nc.scalar.activation(out=get_gq(j)[:, 0, :], in_=flat, func=ACT.Square)
-            if s > 0:
-                nc.scalar.copy(out=get_gq(j)[:, 1, 0:s], in_=flat[:, 0:s])
+            nc.scalar.activation(out=get_gq(j)[:, 0, lo:1024], in_=flat[:, lo:1024], func=ACT.Square)
+
+        def st_cast(j, engine):
+            if not ok(j) or caster(j) != engine:
+                return
+            lo = 512 * first_v(j)
+            flat = qf[j][:].rearrange("p a t m -> p (a t m)")
+            dst = get_gq(j)[:, 1, lo:1024]
+            if engine == "G":
+                nc.gpsimd.tensor_scalar(
+                    out=dst, in0=flat[:, lo:1024], scalar1=1.0, scalar2=0.0, op0=ALU.mult, op1=ALU.add
+                )
+            elif engine == "V":
+                nc.vector.tensor_copy(out=dst, in_=flat[:, lo:1024])
+            else:
+                nc.scalar.copy(out=dst, in_=flat[:, lo:1024])
 
         def st_qq(j):
+            if not ok(j):
+                return
             qc[j] = ring.tile([P, 512], U32, name="qc%d" % j, tag="qc", bufs=4, align_bytes=64)
             qs[j] = ring.tile([P, 512], U8, name="qs%d" % j, tag="qs", bufs=4, align_bytes=64)
             nc.vector.quantize_mx(
@@ -161,6 +212,8 @@ def tile_fuzzy_attention_pa_t_kernel(tc, query, Wq, bq, centers, widths, out):
             )
 
         def st_m2(j):
+            if not ok(j):
+                return
             zb[j] = psum.tile([P, 2, R], F32, name="zb%d" % j, tag="Z", bufs=2)
             for a in range(2):
                 for k in range(2):
@@ -176,6 +229,8 @@ def tile_fuzzy_attention_pa_t_kernel(tc, query, Wq, bq, centers, widths, out):
                     )
 
         def st_z(j):
+            if not ok(j):
+                return
             h = 2 * (j % 2)
             nc.vector.scalar_tensor_tensor(
                 out=zs[j // 2][:, h:h + 2, :],
@@ -227,27 +282,45 @@ def tile_fuzzy_attention_pa_t_kernel(tc, query, Wq, bq, centers, widths, out):
         st_qx(1)
         st_m1(0)
         nc.scalar.activation(out=w2[:], in_=perm(w_sb), func=ACT.Square)
-        for j in range(2, LEAD_T):
-            st_t(j)
-            st_x(j)
-        for j in range(2, LEAD_Q):
-            st_qx(j)
+        nc.vector.reciprocal(out=iw[:], in_=w2[:])
+        nc.vector.tensor_tensor(out=ciw[:], in0=perm(c_sb), in1=iw[:], op=ALU.mult)
+        st_t(2)
+        st_x(2)
+        st_t(3)
+        st_x(3)
+        st_qx(2)
+        st_m1(1)
+        for k in range(2):
+            st_rt(k)
+        for k in range(2):
+            st_rx(k)
+        for k in range(2, 4):
+            st_rt(k)
+        for k in range(2, 4):
+            st_rx(k)
 
-        m2_at = {}
-        for j in range(NPAIR):
-            s = max(j + LAG_M2, FIRST_M2_STEP)
-            m2_at[s] = m2_at.get(s, []) + [j]
+        for q in range(NQUAD + 2):
+            e = 2 * q
+            o = e + 1
+            st_t(e + 4)
+            st_pv(e)
+            st_cast(e, "V")
+            st_sqs(e)
+            st_sq(e)
+            st_cast(e, "S")
 
-        for s in range(NPAIR + LAG_M2 + 1):
-            if s + LEAD_T < NPAIR:
-                st_t(s + LEAD_T)
-            if s == 1:
-                st_rt(0)
-                st_rt(1)
-            if s == 2:
-                st_rt(2)
-                st_rt(3)
-            if s == 4:
+            st_qq(o - 2)
+            st_qx(e + 3)
+            st_cast(e, "G")
+            if q == 0:
+                nc.vector.quantize_mx(
+                    out=rc[:].bitcast(FP8X4), scales=rs[:], in_=rg[:].rearrange("p k r m -> p (k r m)")
+                )
+                nc.vector.tensor_tensor(out=t1[:], in0=perm(c_sb), in1=ciw[:], op=ALU.mult)
+                for t in range(2):
+                    nc.scalar.activation(
+                        out=t1[:, t], in_=t1[:, t], func=ACT.Copy, accum_out=cc[:, t:t + 1]
+                    )
                 ccp = psum.tile([P, R], F32, name="ccp", tag="Z", bufs=2)
                 for t in range(2):
                     nc.tensor.matmul(
@@ -258,40 +331,24 @@ def tile_fuzzy_attention_pa_t_kernel(tc, query, Wq, bq, centers, widths, out):
                         stop=True,
                     )
                 nc.scalar.activation(out=ccs[:], in_=ccp[:], func=ACT.Copy, scale=SCALE)
-            for j in m2_at.get(s, []):
-                st_m2(j)
-            if s + 1 < NPAIR:
-                st_m1(s + 1)
-            if s < NPAIR:
-                st_p(s)
-            if s == 0:
-                nc.vector.reciprocal(out=iw[:], in_=w2[:])
-                nc.gpsimd.tensor_tensor(out=ciw[:], in0=perm(c_sb), in1=iw[:], op=ALU.mult)
-                nc.gpsimd.tensor_tensor(out=t1[:], in0=perm(c_sb), in1=ciw[:], op=ALU.mult)
-            if 0 <= s - LAG_QQ < NPAIR:
-                st_qq(s - LAG_QQ)
-            if s < NPAIR:
-                st_cv(s)
-            for j in m2_at.get(s, []):
-                st_z(j)
-            if s + LEAD_Q < NPAIR:
-                st_qx(s + LEAD_Q)
-            if s == 3:
-                nc.vector.quantize_mx(
-                    out=rc[:].bitcast(FP8X4), scales=rs[:], in_=rg[:].rearrange("p k r m -> p (k r m)")
-                )
-            if s < NPAIR:
-                st_sq(s)
-            if s == 1:
-                st_rx(0)
-                st_rx(1)
-            if s == 2:
-                st_rx(2)
-                st_rx(3)
-            if s == 3:
-                for t in range(2):
-                    nc.scalar.activation(
-                        out=t1[:, t], in_=t1[:, t], func=ACT.Copy, accum_out=cc[:, t:t + 1]
-                    )
-            if s + LEAD_T < NPAIR:
-                st_x(s + LEAD_T)
+            st_m1(e + 2)
+            st_ps(e + 2)
+            st_m2(o - 2)
+            st_x(e + 4)
+            st_t(o + 4)
+
+            st_z(e - 2)
+            st_z(o - 2)
+            st_pv(o)
+            st_cast(o, "V")
+            st_sqs(o)
+            st_sq(o)
+            st_cast(o, "S")
+
+            st_qq(e)
+            st_qx(o + 3)
+            st_cast(o, "G")
+            st_m1(o + 2)
+            st_m2(e)
+            st_ps(o + 2)
+            st_x(o + 4)

@@ -21,9 +21,9 @@ SCALE = -(0.5 / D)
 FLOPS = 2 * TOKENS * D * D + 2 * 2 * TOKENS * D * R
 
 S_FIRST = 3
-S_LAST = 29
-G_FIRST = 2
-G_LAST = 29
+S_LAST = 31
+G_FIRST = 0
+G_LAST = 31
 
 
 def s_tile(j):
@@ -277,50 +277,25 @@ def tile_fuzzy_attention_pa_t_kernel(tc, query, Wq, bq, centers, widths, out):
         nc.vector.tensor_copy(out=wgv[:, 2:4], in_=twb[1][:].rearrange("p m u c -> p m c u"))
         st_qx(0)
         nc.vector.quantize_mx(out=wc[:].bitcast(FP8X4), scales=ws[:], in_=wg[:])
+        nc.scalar.activation(out=w2[:], in_=perm(w_sb), func=ACT.Square)
         st_t(1)
         st_x(1)
+        nc.vector.reciprocal(out=iw[:], in_=w2[:])
         st_qx(1)
         st_m1(0)
-        nc.scalar.activation(out=w2[:], in_=perm(w_sb), func=ACT.Square)
-        nc.vector.reciprocal(out=iw[:], in_=w2[:])
-        nc.vector.tensor_tensor(out=ciw[:], in0=perm(c_sb), in1=iw[:], op=ALU.mult)
         st_t(2)
-        st_x(2)
         st_t(3)
+        st_x(2)
         st_x(3)
-        st_qx(2)
+        st_rt(0)
+        st_rt(1)
         st_m1(1)
-        for k in range(2):
-            st_rt(k)
-        for k in range(2):
-            st_rx(k)
-        for k in range(2, 4):
-            st_rt(k)
-        for k in range(2, 4):
-            st_rx(k)
 
         for q in range(NQUAD + 2):
             e = 2 * q
             o = e + 1
             st_t(e + 4)
-            st_pv(e)
-            st_cast(e, "V")
-            st_sqs(e)
-            st_sq(e)
-            st_cast(e, "S")
-
-            st_qq(o - 2)
-            st_qx(e + 3)
-            st_cast(e, "G")
-            if q == 0:
-                nc.vector.quantize_mx(
-                    out=rc[:].bitcast(FP8X4), scales=rs[:], in_=rg[:].rearrange("p k r m -> p (k r m)")
-                )
-                nc.vector.tensor_tensor(out=t1[:], in0=perm(c_sb), in1=ciw[:], op=ALU.mult)
-                for t in range(2):
-                    nc.scalar.activation(
-                        out=t1[:, t], in_=t1[:, t], func=ACT.Copy, accum_out=cc[:, t:t + 1]
-                    )
+            if q == 1:
                 ccp = psum.tile([P, R], F32, name="ccp", tag="Z", bufs=2)
                 for t in range(2):
                     nc.tensor.matmul(
@@ -330,20 +305,48 @@ def tile_fuzzy_attention_pa_t_kernel(tc, query, Wq, bq, centers, widths, out):
                         start=True,
                         stop=True,
                     )
+            st_pv(e)
+            if q == 0:
+                nc.vector.tensor_tensor(out=ciw[:], in0=perm(c_sb), in1=iw[:], op=ALU.mult)
+                st_qx(2)
+            st_sqs(e)
+            st_sq(e)
+            if q == 0:
+                st_rx(0)
+                st_rx(1)
+            if q == 1:
                 nc.scalar.activation(out=ccs[:], in_=ccp[:], func=ACT.Copy, scale=SCALE)
+
+            st_qq(o - 2)
+            st_qx(e + 3)
+            st_cast(e, "G")
+            if q == 0:
+                st_rt(2)
+                st_rt(3)
             st_m1(e + 2)
             st_ps(e + 2)
-            st_m2(o - 2)
             st_x(e + 4)
             st_t(o + 4)
+            if q == 0:
+                st_rx(2)
+                st_rx(3)
 
+            st_z(o - 4)
             st_z(e - 2)
-            st_z(o - 2)
+            st_m2(o - 2)
             st_pv(o)
-            st_cast(o, "V")
+            if q == 0:
+                nc.vector.tensor_tensor(out=t1[:], in0=perm(c_sb), in1=ciw[:], op=ALU.mult)
+                nc.vector.quantize_mx(
+                    out=rc[:].bitcast(FP8X4), scales=rs[:], in_=rg[:].rearrange("p k r m -> p (k r m)")
+                )
             st_sqs(o)
             st_sq(o)
-            st_cast(o, "S")
+            if q == 0:
+                for t in range(2):
+                    nc.scalar.activation(
+                        out=t1[:, t], in_=t1[:, t], func=ACT.Copy, accum_out=cc[:, t:t + 1]
+                    )
 
             st_qq(e)
             st_qx(o + 3)

@@ -146,7 +146,7 @@ def tile_fuzzy_attention_pa_t_kernel(tc, query, Wq, bq, centers, widths, out):
         def st_pv(j):
             if not ok(j):
                 return
-            qf[j] = ring.tile([P, 2, P, 4], F32, name="qf%d" % j, tag="qf", bufs=4)
+            qf[j] = ring.tile([P, 2, P, 4], F32, name="qf%d" % j, tag="qf", bufs=3)
             for a in range(first_v(j), 2):
                 nc.vector.tensor_tensor(
                     out=qf[j][:, a, :, :],
@@ -166,7 +166,7 @@ def tile_fuzzy_attention_pa_t_kernel(tc, query, Wq, bq, centers, widths, out):
 
         def get_gq(j):
             if j not in gq:
-                gq[j] = ring.tile([P, 2, 1024], BF16, name="gq%d" % j, tag="gq", bufs=4, align_bytes=64)
+                gq[j] = ring.tile([P, 2, 1024], BF16, name="gq%d" % j, tag="gq", bufs=2, align_bytes=64)
             return gq[j]
 
         def st_sqs(j):
@@ -309,37 +309,41 @@ def tile_fuzzy_attention_pa_t_kernel(tc, query, Wq, bq, centers, widths, out):
             if q == 0:
                 nc.vector.tensor_tensor(out=ciw[:], in0=perm(c_sb), in1=iw[:], op=ALU.mult)
                 st_qx(2)
-            st_sqs(e)
+            st_x(e + 4)
+            st_ps(o)
+
+            st_qx(e + 3)
+            st_qq(e - 2)
+            st_cast(e, "G")
             st_sq(e)
             if q == 0:
                 st_rx(0)
                 st_rx(1)
             if q == 1:
                 nc.scalar.activation(out=ccs[:], in_=ccp[:], func=ACT.Copy, scale=SCALE)
-
-            st_qq(o - 2)
-            st_qx(e + 3)
-            st_cast(e, "G")
+            st_m1(e + 2)
+            st_t(o + 4)
             if q == 0:
                 st_rt(2)
                 st_rt(3)
-            st_m1(e + 2)
-            st_ps(e + 2)
-            st_x(e + 4)
-            st_t(o + 4)
-            if q == 0:
                 st_rx(2)
                 st_rx(3)
 
+            st_z(e - 4)
             st_z(o - 4)
-            st_z(e - 2)
-            st_m2(o - 2)
+            st_m2(e - 2)
             st_pv(o)
             if q == 0:
                 nc.vector.tensor_tensor(out=t1[:], in0=perm(c_sb), in1=ciw[:], op=ALU.mult)
+            st_x(o + 4)
+
+            st_qx(o + 3)
+            st_qq(o - 2)
+            if q == 0:
                 nc.vector.quantize_mx(
                     out=rc[:].bitcast(FP8X4), scales=rs[:], in_=rg[:].rearrange("p k r m -> p (k r m)")
                 )
+            st_cast(o, "G")
             st_sqs(o)
             st_sq(o)
             if q == 0:
@@ -347,11 +351,5 @@ def tile_fuzzy_attention_pa_t_kernel(tc, query, Wq, bq, centers, widths, out):
                     nc.scalar.activation(
                         out=t1[:, t], in_=t1[:, t], func=ACT.Copy, accum_out=cc[:, t:t + 1]
                     )
-
-            st_qq(e)
-            st_qx(o + 3)
-            st_cast(o, "G")
             st_m1(o + 2)
-            st_m2(e)
-            st_ps(o + 2)
-            st_x(o + 4)
+            st_m2(o - 2)

@@ -63,6 +63,10 @@ def tile_fuzzy_attention_pa_t_kernel(tc, query, Wq, bq, centers, widths, out):
         for j in range(1, NQUAD):
             nc.sync.dma_start(out=x_sb[j][:], in_=xv[j])
 
+        one = const.tile([P, 1], F32, name="one")
+        warm = const.tile([P, 1], F32, name="warm")
+        nc.vector.memset(one[:], 1.0)
+        nc.scalar.activation(out=warm[:], in_=one[:], func=ACT.Abs_reciprocal_sqrt)
         ident = const.tile([P, P], F32, name="ident")
         make_identity(nc, ident[:])
         bias = const.tile([P, 4], F32, name="bias")
@@ -72,6 +76,9 @@ def tile_fuzzy_attention_pa_t_kernel(tc, query, Wq, bq, centers, widths, out):
         wc = const.tile([P, 512], U32, name="wc", align_bytes=64)
         ws = const.tile([P, 512], U8, name="ws", align_bytes=64)
         w2 = const.tile([P, 2, 4, P], F32, name="w2")
+        r0 = const.tile([P, 2, 4, P], F32, name="r0")
+        y0 = const.tile([P, 2, 4, P], F32, name="y0")
+        t0 = const.tile([P, 2, 4, P], F32, name="t0")
         iw = const.tile([P, 2, 4, P], F32, name="iw")
         ciw = const.tile([P, 2, 4, P], F32, name="ciw")
         t1 = const.tile([P, 2, 4, P], F32, name="t1")
@@ -259,8 +266,11 @@ def tile_fuzzy_attention_pa_t_kernel(tc, query, Wq, bq, centers, widths, out):
                 out=rg[:, k // 2, (k % 2) * P:(k % 2 + 1) * P, :],
                 in_=rtb[k][:].rearrange("p m r -> p r m"),
                 func=ACT.Copy,
-                scale=(1.0 if k < 2 else -2.0),
+                scale=(-1.0 if k < 2 else 2.0),
             )
+
+        def flat(t):
+            return t[:].rearrange("p t m c -> p (t m c)")
 
         st_t(0)
         st_x(0)
@@ -280,21 +290,47 @@ def tile_fuzzy_attention_pa_t_kernel(tc, query, Wq, bq, centers, widths, out):
         nc.scalar.activation(out=w2[:], in_=perm(w_sb), func=ACT.Square)
         st_t(1)
         st_x(1)
-        nc.vector.reciprocal(out=iw[:], in_=w2[:])
+        nc.scalar.activation(out=r0[:], in_=w2[:], func=ACT.Abs_reciprocal_sqrt)
+        nc.scalar.activation(out=y0[:], in_=r0[:], func=ACT.Square)
         st_qx(1)
         st_m1(0)
         st_t(2)
         st_t(3)
         st_x(2)
         st_x(3)
-        st_rt(0)
-        st_rt(1)
         st_m1(1)
 
         for q in range(NQUAD + 2):
             e = 2 * q
             o = e + 1
             st_t(e + 4)
+            st_pv(e)
+            if q == 0:
+                st_qx(2)
+                nc.vector.tensor_tensor(out=t0[:], in0=w2[:], in1=y0[:], op=ALU.mult)
+                nc.vector.scalar_tensor_tensor(
+                    out=flat(iw), in0=flat(t0), scalar=2.0, in1=flat(y0), op0=ALU.subtract, op1=ALU.mult
+                )
+            st_x(e + 4)
+            st_ps(o)
+
+            st_qx(e + 3)
+            st_qq(e - 2)
+            if q == 0:
+                nc.vector.tensor_tensor(out=ciw[:], in0=perm(c_sb), in1=iw[:], op=ALU.mult)
+            if q == 1:
+                nc.vector.quantize_mx(
+                    out=rc[:].bitcast(FP8X4), scales=rs[:], in_=rg[:].rearrange("p k r m -> p (k r m)")
+                )
+            st_cast(e, "G")
+            st_sq(e)
+            st_m1(e + 2)
+            st_t(o + 4)
+            if q == 0:
+                st_rt(0)
+                st_rt(1)
+                st_rx(0)
+                st_rx(1)
             if q == 1:
                 ccp = psum.tile([P, R], F32, name="ccp", tag="Z", bufs=2)
                 for t in range(2):
@@ -305,44 +341,25 @@ def tile_fuzzy_attention_pa_t_kernel(tc, query, Wq, bq, centers, widths, out):
                         start=True,
                         stop=True,
                     )
-            st_pv(e)
-            if q == 0:
-                nc.vector.tensor_tensor(out=ciw[:], in0=perm(c_sb), in1=iw[:], op=ALU.mult)
-                st_qx(2)
-            st_x(e + 4)
-            st_ps(o)
-
-            st_qx(e + 3)
-            st_qq(e - 2)
-            st_cast(e, "G")
-            st_sq(e)
-            if q == 0:
-                st_rx(0)
-                st_rx(1)
-            if q == 1:
-                nc.scalar.activation(out=ccs[:], in_=ccp[:], func=ACT.Copy, scale=SCALE)
-            st_m1(e + 2)
-            st_t(o + 4)
-            if q == 0:
-                st_rt(2)
-                st_rt(3)
-                st_rx(2)
-                st_rx(3)
 
             st_z(e - 4)
             st_z(o - 4)
             st_m2(e - 2)
+            if q == 0:
+                st_rt(2)
+                st_rt(3)
             st_pv(o)
             if q == 0:
                 nc.vector.tensor_tensor(out=t1[:], in0=perm(c_sb), in1=ciw[:], op=ALU.mult)
             st_x(o + 4)
+            if q == 0:
+                st_rx(2)
+                st_rx(3)
+            if q == 1:
+                nc.scalar.activation(out=ccs[:], in_=ccp[:], func=ACT.Copy, scale=-SCALE)
 
             st_qx(o + 3)
             st_qq(o - 2)
-            if q == 0:
-                nc.vector.quantize_mx(
-                    out=rc[:].bitcast(FP8X4), scales=rs[:], in_=rg[:].rearrange("p k r m -> p (k r m)")
-                )
             st_cast(o, "G")
             st_sqs(o)
             st_sq(o)

@@ -22,8 +22,6 @@ FLOPS = 2 * TOKENS * D * D + 2 * 2 * TOKENS * D * R
 
 S_FIRST = 3
 S_LAST = 31
-G_FIRST = 0
-G_LAST = 31
 
 
 def s_tile(j):
@@ -31,11 +29,7 @@ def s_tile(j):
 
 
 def caster(j):
-    if j < G_FIRST:
-        return "S"
-    if j > G_LAST:
-        return "V"
-    return "G"
+    return "S" if s_tile(j) else "G"
 
 
 def tile_fuzzy_attention_pa_t_kernel(tc, query, Wq, bq, centers, widths, out):
@@ -77,8 +71,6 @@ def tile_fuzzy_attention_pa_t_kernel(tc, query, Wq, bq, centers, widths, out):
         ws = const.tile([P, 512], U8, name="ws", align_bytes=64)
         w2 = const.tile([P, 2, 4, P], F32, name="w2")
         r0 = const.tile([P, 2, 4, P], F32, name="r0")
-        y0 = const.tile([P, 2, 4, P], F32, name="y0")
-        t0 = const.tile([P, 2, 4, P], F32, name="t0")
         iw = const.tile([P, 2, 4, P], F32, name="iw")
         ciw = const.tile([P, 2, 4, P], F32, name="ciw")
         t1 = const.tile([P, 2, 4, P], F32, name="t1")
@@ -183,7 +175,14 @@ def tile_fuzzy_attention_pa_t_kernel(tc, query, Wq, bq, centers, widths, out):
             nc.scalar.activation(
                 out=get_gq(j)[:, 0, 0:512].rearrange("p (t m) -> p t m", m=4), in_=src, func=ACT.Square
             )
-            nc.scalar.copy(out=get_gq(j)[:, 1, 0:512].rearrange("p (t m) -> p t m", m=4), in_=src)
+            nc.gpsimd.tensor_scalar(
+                out=get_gq(j)[:, 1, 0:512].rearrange("p (t m) -> p t m", m=4),
+                in0=src,
+                scalar1=1.0,
+                scalar2=0.0,
+                op0=ALU.mult,
+                op1=ALU.add,
+            )
 
         def st_sq(j):
             if not ok(j):
@@ -266,11 +265,8 @@ def tile_fuzzy_attention_pa_t_kernel(tc, query, Wq, bq, centers, widths, out):
                 out=rg[:, k // 2, (k % 2) * P:(k % 2 + 1) * P, :],
                 in_=rtb[k][:].rearrange("p m r -> p r m"),
                 func=ACT.Copy,
-                scale=(-1.0 if k < 2 else 2.0),
+                scale=(1.0 if k < 2 else -2.0),
             )
-
-        def flat(t):
-            return t[:].rearrange("p t m c -> p (t m c)")
 
         st_t(0)
         st_x(0)
@@ -291,7 +287,7 @@ def tile_fuzzy_attention_pa_t_kernel(tc, query, Wq, bq, centers, widths, out):
         st_t(1)
         st_x(1)
         nc.scalar.activation(out=r0[:], in_=w2[:], func=ACT.Abs_reciprocal_sqrt)
-        nc.scalar.activation(out=y0[:], in_=r0[:], func=ACT.Square)
+        nc.scalar.activation(out=iw[:], in_=r0[:], func=ACT.Square)
         st_qx(1)
         st_m1(0)
         st_t(2)
@@ -307,17 +303,23 @@ def tile_fuzzy_attention_pa_t_kernel(tc, query, Wq, bq, centers, widths, out):
             st_pv(e)
             if q == 0:
                 st_qx(2)
-                nc.vector.tensor_tensor(out=t0[:], in0=w2[:], in1=y0[:], op=ALU.mult)
-                nc.vector.scalar_tensor_tensor(
-                    out=flat(iw), in0=flat(t0), scalar=2.0, in1=flat(y0), op0=ALU.subtract, op1=ALU.mult
-                )
+                nc.vector.tensor_tensor(out=ciw[:], in0=perm(c_sb), in1=iw[:], op=ALU.mult)
             st_x(e + 4)
             st_ps(o)
 
             st_qx(e + 3)
             st_qq(e - 2)
             if q == 0:
-                nc.vector.tensor_tensor(out=ciw[:], in0=perm(c_sb), in1=iw[:], op=ALU.mult)
+                for t in range(2):
+                    nc.vector.scalar_tensor_tensor(
+                        out=t1[:, t],
+                        in0=perm(c_sb)[:, t],
+                        scalar=1.0,
+                        in1=ciw[:, t],
+                        op0=ALU.mult,
+                        op1=ALU.mult,
+                        accum_out=cc[:, t:t + 1],
+                    )
             if q == 1:
                 nc.vector.quantize_mx(
                     out=rc[:].bitcast(FP8X4), scales=rs[:], in_=rg[:].rearrange("p k r m -> p (k r m)")
@@ -349,24 +351,18 @@ def tile_fuzzy_attention_pa_t_kernel(tc, query, Wq, bq, centers, widths, out):
                 st_rt(2)
                 st_rt(3)
             st_pv(o)
-            if q == 0:
-                nc.vector.tensor_tensor(out=t1[:], in0=perm(c_sb), in1=ciw[:], op=ALU.mult)
             st_x(o + 4)
             if q == 0:
                 st_rx(2)
                 st_rx(3)
             if q == 1:
-                nc.scalar.activation(out=ccs[:], in_=ccp[:], func=ACT.Copy, scale=-SCALE)
+                nc.scalar.activation(out=ccs[:], in_=ccp[:], func=ACT.Copy, scale=SCALE)
 
             st_qx(o + 3)
             st_qq(o - 2)
             st_cast(o, "G")
             st_sqs(o)
             st_sq(o)
-            if q == 0:
-                for t in range(2):
-                    nc.scalar.activation(
-                        out=t1[:, t], in_=t1[:, t], func=ACT.Copy, accum_out=cc[:, t:t + 1]
-                    )
+            st_cast(o, "S")
             st_m1(o + 2)
             st_m2(o - 2)

@@ -307,8 +307,8 @@ def tile_fuzzy_attention_pa_t_kernel(tc, query, Wq, bq, centers, widths, out):
             st_x(e + 4)
             st_ps(o)
 
-            st_qx(e + 3)
             st_qq(e - 2)
+            st_qx(e + 3)
             if q == 0:
                 for t in range(2):
                     nc.vector.scalar_tensor_tensor(
@@ -358,8 +358,8 @@ def tile_fuzzy_attention_pa_t_kernel(tc, query, Wq, bq, centers, widths, out):
             if q == 1:
                 nc.scalar.activation(out=ccs[:], in_=ccp[:], func=ACT.Copy, scale=SCALE)
 
-            st_qx(o + 3)
             st_qq(o - 2)
+            st_qx(o + 3)
             st_cast(o, "G")
             st_sqs(o)
             st_sq(o)

@@ -302,6 +302,7 @@ def tile_fuzzy_attention_pa_t_kernel(tc, query, Wq, bq, centers, widths, out):
             st_t(e + 4)
             st_pv(e)
             if q == 0:
+                st_pv(1)
                 st_qx(2)
                 nc.vector.tensor_tensor(out=ciw[:], in0=perm(c_sb), in1=iw[:], op=ALU.mult)
             st_x(e + 4)
@@ -350,7 +351,8 @@ def tile_fuzzy_attention_pa_t_kernel(tc, query, Wq, bq, centers, widths, out):
             if q == 0:
                 st_rt(2)
                 st_rt(3)
-            st_pv(o)
+            if q > 0:
+                st_pv(o)
             st_x(o + 4)
             if q == 0:
                 st_rx(2)

@@ -20,16 +20,12 @@ NPAIR = TOKENS // 256
 SCALE = -(0.5 / D)
 FLOPS = 2 * TOKENS * D * D + 2 * 2 * TOKENS * D * R
 
-S_FIRST = 3
-S_LAST = 31
+
+S_FROM = 4
 
 
-def s_tile(j):
-    return j % 2 == 1 and S_FIRST <= j <= S_LAST
-
-
-def caster(j):
-    return "S" if s_tile(j) else "G"
+def s_pair(j):
+    return j % 3 == 1 and j >= S_FROM
 
 
 def tile_fuzzy_attention_pa_t_kernel(tc, query, Wq, bq, centers, widths, out):
@@ -48,12 +44,14 @@ def tile_fuzzy_attention_pa_t_kernel(tc, query, Wq, bq, centers, widths, out):
         bq_sb = const.tile([P, 4], BF16, name="bq_sb")
         w_sb = const.tile([P, 2, D], BF16, name="w_sb")
         c_sb = const.tile([P, 2, D], BF16, name="c_sb")
+        wqv = Wq.rearrange("(c m) i -> c m i", m=4)
+        nc.sync.dma_start(out=wq_sb[:, 0:2, :], in_=wqv[:, 0:2, :])
+        nc.sync.dma_start(out=wq_sb[:, 2:4, :], in_=wqv[:, 2:4, :])
         nc.sync.dma_start(out=x_sb[0][:, 0:2, :], in_=xv[0][:, 0:2, :])
-        nc.sync.dma_start(out=wq_sb[:], in_=Wq.rearrange("(c m) i -> c m i", m=4))
+        nc.sync.dma_start(out=x_sb[0][:, 2:4, :], in_=xv[0][:, 2:4, :])
         nc.sync.dma_start(out=bq_sb[:], in_=bq.rearrange("(c m) -> c m", m=4))
         nc.sync.dma_start(out=w_sb[:], in_=widths.rearrange("(t p) d -> p t d", p=P))
         nc.sync.dma_start(out=c_sb[:], in_=centers.rearrange("(t p) d -> p t d", p=P))
-        nc.sync.dma_start(out=x_sb[0][:, 2:4, :], in_=xv[0][:, 2:4, :])
         for j in range(1, NQUAD):
             nc.sync.dma_start(out=x_sb[j][:], in_=xv[j])
 
@@ -63,18 +61,18 @@ def tile_fuzzy_attention_pa_t_kernel(tc, query, Wq, bq, centers, widths, out):
         nc.scalar.activation(out=warm[:], in_=one[:], func=ACT.Abs_reciprocal_sqrt)
         ident = const.tile([P, P], F32, name="ident")
         make_identity(nc, ident[:])
+        ones = const.tile([P, P], F32, name="ones")
+        nc.vector.memset(ones[:], 1.0)
         bias = const.tile([P, 4], F32, name="bias")
-        nc.vector.tensor_copy(out=bias[:], in_=bq_sb[:])
 
         wg = const.tile([P, 2048], BF16, name="wg", align_bytes=64)
         wc = const.tile([P, 512], U32, name="wc", align_bytes=64)
         ws = const.tile([P, 512], U8, name="ws", align_bytes=64)
-        w2 = const.tile([P, 2, 4, P], F32, name="w2")
-        r0 = const.tile([P, 2, 4, P], F32, name="r0")
-        iw = const.tile([P, 2, 4, P], F32, name="iw")
-        ciw = const.tile([P, 2, 4, P], F32, name="ciw")
-        t1 = const.tile([P, 2, 4, P], F32, name="t1")
-        cc = const.tile([P, 2], F32, name="cc")
+        w2 = const.tile([P, R, 4], F32, name="w2")
+        r0 = const.tile([P, R, 4], F32, name="r0")
+        iw = const.tile([P, R, 4], F32, name="iw")
+        ciw = const.tile([P, R, 4], F32, name="ciw")
+        t1 = const.tile([P, R, 4], F32, name="t1")
         ccs = const.tile([P, R], F32, name="ccs")
         rg = const.tile([P, 2, R, 4], BF16, name="rg", align_bytes=64)
         rc = const.tile([P, 512], U32, name="rc", align_bytes=64)
@@ -87,12 +85,10 @@ def tile_fuzzy_attention_pa_t_kernel(tc, query, Wq, bq, centers, widths, out):
         xs = {}
         ab = {}
         qf = {}
-        qfp = {}
         gq = {}
         qc = {}
         qs = {}
         zb = {}
-        rtb = {}
 
         def ok(j):
             return 0 <= j < NPAIR
@@ -115,6 +111,13 @@ def tile_fuzzy_attention_pa_t_kernel(tc, query, Wq, bq, centers, widths, out):
                 in_=tb[j][:].rearrange("p a u t -> p a t u"),
             )
 
+        def st_xv(j):
+            xg[j] = ring.tile([P, 1024], BF16, name="xg%d" % j, tag="xg", bufs=3, align_bytes=64)
+            nc.vector.tensor_copy(
+                out=xg[j][:].bitcast(F32).rearrange("p (a t u) -> p a t u", a=2, u=2),
+                in_=tb[j][:].rearrange("p a u t -> p a t u"),
+            )
+
         def st_qx(j):
             if not ok(j):
                 return
@@ -125,42 +128,43 @@ def tile_fuzzy_attention_pa_t_kernel(tc, query, Wq, bq, centers, widths, out):
         def st_m1(j):
             if not ok(j):
                 return
-            for a in range(2):
-                acc = psum.tile([P, 4, P], F32, name="ab%d_%d" % (j, a), tag="A", bufs=4)
-                ab[(j, a)] = acc
-                for m in range(4):
+            wide = 256 if s_pair(j) else P
+            per = 512 // wide
+            for h in range(2):
+                acc = psum.tile([P, per, wide], F32, name="ab%d_%d" % (j, h), tag="A", bufs=4)
+                ab[(j, h)] = acc
+                for n in range(per):
+                    m = 2 * h + n if s_pair(j) else n
+                    lo = 0 if s_pair(j) else h * P
                     nc.tensor.matmul_mx(
-                        out=acc[:, m, :],
+                        out=acc[:, n, :],
                         lhsT=wc[:, m * P:(m + 1) * P].bitcast(FP8X4),
                         lhsT_scale=ws[:, m * P:(m + 1) * P],
-                        rhs=xc[j][:, a * P:(a + 1) * P].bitcast(FP8X4),
-                        rhs_scale=xs[j][:, a * P:(a + 1) * P],
+                        rhs=xc[j][:, lo:lo + wide].bitcast(FP8X4),
+                        rhs_scale=xs[j][:, lo:lo + wide],
                         start=True,
                         stop=True,
                     )
 
-        def first_v(j):
-            return 1 if s_tile(j) else 0
-
         def st_pv(j):
-            if not ok(j):
+            if not ok(j) or s_pair(j):
                 return
-            qf[j] = ring.tile([P, 2, P, 4], F32, name="qf%d" % j, tag="qf", bufs=3)
-            for a in range(first_v(j), 2):
+            qf[j] = ring.tile([P, 256, 4], F32, name="qf%d" % j, tag="qf", bufs=3)
+            for a in range(2):
                 nc.vector.tensor_tensor(
-                    out=qf[j][:, a, :, :],
+                    out=qf[j][:, a * P:(a + 1) * P, :],
                     in0=ab[(j, a)][:].rearrange("p m t -> p t m"),
                     in1=bias[:].unsqueeze(1).to_broadcast([P, P, 4]),
                     op=ALU.add,
                 )
 
         def st_ps(j):
-            if not ok(j) or not s_tile(j):
+            if not ok(j) or not s_pair(j):
                 return
-            qfp[j] = ring.tile([P, 4, P], F32, name="qfp%d" % j, tag="qfp", bufs=2)
+            qf[j] = ring.tile([P, 4, 256], F32, name="qp%d" % j, tag="qp", bufs=2)
             for m in range(4):
                 nc.scalar.activation(
-                    out=qfp[j][:, m, :], in_=ab[(j, 0)][:, m, :], func=ACT.Identity, bias=bias[:, m:m + 1]
+                    out=qf[j][:, m, :], in_=ab[(j, m // 2)][:, m % 2, :], func=ACT.Identity, bias=bias[:, m:m + 1]
                 )
 
         def get_gq(j):
@@ -168,43 +172,27 @@ def tile_fuzzy_attention_pa_t_kernel(tc, query, Wq, bq, centers, widths, out):
                 gq[j] = ring.tile([P, 2, 1024], BF16, name="gq%d" % j, tag="gq", bufs=2, align_bytes=64)
             return gq[j]
 
-        def st_sqs(j):
-            if not ok(j) or not s_tile(j):
-                return
-            src = qfp[j][:].rearrange("p m t -> p t m")
-            nc.scalar.activation(
-                out=get_gq(j)[:, 0, 0:512].rearrange("p (t m) -> p t m", m=4), in_=src, func=ACT.Square
-            )
-            nc.gpsimd.tensor_scalar(
-                out=get_gq(j)[:, 1, 0:512].rearrange("p (t m) -> p t m", m=4),
-                in0=src,
-                scalar1=1.0,
-                scalar2=0.0,
-                op0=ALU.mult,
-                op1=ALU.add,
-            )
+        def views(j, k):
+            if s_pair(j):
+                dst = get_gq(j)[:, k, :].rearrange("p (c i m) -> p c m i", i=4, m=4)
+                return dst, qf[j][:].rearrange("p m (c i) -> p c m i", i=4)
+            return get_gq(j)[:, k, :], qf[j][:].rearrange("p t m -> p (t m)")
 
         def st_sq(j):
             if not ok(j):
                 return
-            lo = 512 * first_v(j)
-            flat = qf[j][:].rearrange("p a t m -> p (a t m)")
-            nc.scalar.activation(out=get_gq(j)[:, 0, lo:1024], in_=flat[:, lo:1024], func=ACT.Square)
+            dst, src = views(j, 0)
+            nc.scalar.activation(out=dst, in_=src, func=ACT.Square)
 
-        def st_cast(j, engine):
-            if not ok(j) or caster(j) != engine:
+        def st_cast(j):
+            if not ok(j):
                 return
-            lo = 512 * first_v(j)
-            flat = qf[j][:].rearrange("p a t m -> p (a t m)")
-            dst = get_gq(j)[:, 1, lo:1024]
-            if engine == "G":
-                nc.gpsimd.tensor_scalar(
-                    out=dst, in0=flat[:, lo:1024], scalar1=1.0, scalar2=0.0, op0=ALU.mult, op1=ALU.add
-                )
-            elif engine == "V":
-                nc.vector.tensor_copy(out=dst, in_=flat[:, lo:1024])
-            else:
-                nc.scalar.copy(out=dst, in_=flat[:, lo:1024])
+            dst, src = views(j, 1)
+            nc.gpsimd.tensor_scalar(out=dst, in0=src, scalar1=1.0, scalar2=0.0, op0=ALU.mult, op1=ALU.add)
+
+        def st_castv(j):
+            dst, src = views(j, 1)
+            nc.vector.tensor_copy(out=dst, in_=src)
 
         def st_qq(j):
             if not ok(j):
@@ -251,25 +239,23 @@ def tile_fuzzy_attention_pa_t_kernel(tc, query, Wq, bq, centers, widths, out):
             elif j % 2 == 1:
                 nc.sync.dma_start(out=ov[j // 2], in_=zs[j // 2][:])
 
-        def perm(t):
-            return t[:].rearrange("p t (c m) -> p t m c", m=4)
+        def rule_t(src, name, tag):
+            bank = psum.tile([P, 2, R], F32, name=name, tag=tag, bufs=4 if tag == "A" else 2)
+            for t in range(2):
+                words = src[:, t, :].bitcast(F32)
+                for u in range(2):
+                    nc.tensor.transpose(bank[:, u, t * P:(t + 1) * P], words[:, u:2 * P:2], ident[:])
+            return bank
 
-        def st_rt(k):
-            src = iw if k < 2 else ciw
-            rtb[k] = psum.tile([P, 4, P], F32, name="rtb%d" % k, tag="Z", bufs=2)
-            for m in range(4):
-                nc.tensor.transpose(rtb[k][:, m, :], src[:, k % 2, m, :], ident[:])
+        def pairs(bank):
+            return bank[:].rearrange("p u r -> p (u r)").bitcast(BF16).rearrange("p (u r e) -> p r u e", u=2, e=2)
 
-        def st_rx(k):
-            nc.scalar.activation(
-                out=rg[:, k // 2, (k % 2) * P:(k % 2 + 1) * P, :],
-                in_=rtb[k][:].rearrange("p m r -> p r m"),
-                func=ACT.Copy,
-                scale=(1.0 if k < 2 else -2.0),
-            )
+        def quad4(t):
+            return t[:].rearrange("p r (u e) -> p r u e", u=2)
 
-        st_t(0)
-        st_x(0)
+        def flat(t):
+            return t[:].rearrange("p r m -> p (r m)")
+
         twb = []
         for h in range(2):
             t = psum.tile([P, 2, 2, P], F32, name="twb%d" % h, tag="A", bufs=4)
@@ -278,93 +264,74 @@ def tile_fuzzy_attention_pa_t_kernel(tc, query, Wq, bq, centers, widths, out):
                 words = wq_sb[:, 2 * h + m, :].bitcast(F32)
                 for u in range(2):
                     nc.tensor.transpose(t[:, m, u, :], words[:, u * P:(u + 1) * P], ident[:])
-        wgv = wg[:].bitcast(F32).rearrange("p (m c u) -> p m c u", m=4, u=2)
-        nc.scalar.copy(out=wgv[:, 0:2], in_=twb[0][:].rearrange("p m u c -> p m c u"))
-        nc.vector.tensor_copy(out=wgv[:, 2:4], in_=twb[1][:].rearrange("p m u c -> p m c u"))
-        st_qx(0)
-        nc.vector.quantize_mx(out=wc[:].bitcast(FP8X4), scales=ws[:], in_=wg[:])
-        nc.scalar.activation(out=w2[:], in_=perm(w_sb), func=ACT.Square)
+        st_t(0)
         st_t(1)
+        wT = rule_t(w_sb, "wT", "Z")
+        wgv = wg[:].bitcast(F32).rearrange("p (m c u) -> p m c u", m=4, u=2)
+        nc.vector.tensor_copy(out=wgv[:, 0:2], in_=twb[0][:].rearrange("p m u c -> p m c u"))
+        nc.scalar.copy(out=wgv[:, 2:4], in_=twb[1][:].rearrange("p m u c -> p m c u"))
+        st_x(0)
+        for h in range(2):
+            nc.vector.quantize_mx(out=wc[:, 256 * h:256 * h + 256].bitcast(FP8X4), scales=ws[:, 256 * h:256 * h + 256], in_=wg[:, 1024 * h:1024 * h + 1024])
+        st_qx(0)
+        st_m1(0)
+        nc.vector.tensor_copy(out=bias[:], in_=bq_sb[:])
         st_x(1)
+        st_qx(1)
+        nc.scalar.activation(out=quad4(w2), in_=pairs(wT), func=ACT.Square)
+        st_m1(1)
+        st_t(2)
+        cB = rule_t(c_sb, "cB", "Z")
+        st_t(3)
         nc.scalar.activation(out=r0[:], in_=w2[:], func=ACT.Abs_reciprocal_sqrt)
         nc.scalar.activation(out=iw[:], in_=r0[:], func=ACT.Square)
-        st_qx(1)
-        st_m1(0)
-        st_t(2)
-        st_t(3)
-        st_x(2)
-        st_x(3)
-        st_m1(1)
 
-        for q in range(NQUAD + 2):
-            e = 2 * q
-            o = e + 1
-            st_t(e + 4)
-            st_pv(e)
-            if q == 0:
-                st_pv(1)
-                st_qx(2)
-                nc.vector.tensor_tensor(out=ciw[:], in0=perm(c_sb), in1=iw[:], op=ALU.mult)
-            st_x(e + 4)
-            st_ps(o)
-
-            st_qq(e - 2)
-            st_qx(e + 3)
-            if q == 0:
-                for t in range(2):
-                    nc.vector.scalar_tensor_tensor(
-                        out=t1[:, t],
-                        in0=perm(c_sb)[:, t],
-                        scalar=1.0,
-                        in1=ciw[:, t],
-                        op0=ALU.mult,
-                        op1=ALU.mult,
-                        accum_out=cc[:, t:t + 1],
-                    )
-            if q == 1:
-                nc.vector.quantize_mx(
-                    out=rc[:].bitcast(FP8X4), scales=rs[:], in_=rg[:].rearrange("p k r m -> p (k r m)")
-                )
-            st_cast(e, "G")
-            st_sq(e)
-            st_m1(e + 2)
-            st_t(o + 4)
-            if q == 0:
-                st_rt(0)
-                st_rt(1)
-                st_rx(0)
-                st_rx(1)
-            if q == 1:
+        for s in range(NPAIR + 5):
+            r = (s + 1) % 3
+            g = s - r
+            if s > 1:
+                st_t(s + 4)
+            if s == 2:
                 ccp = psum.tile([P, R], F32, name="ccp", tag="Z", bufs=2)
-                for t in range(2):
-                    nc.tensor.matmul(
-                        out=ccp[:, t * P:(t + 1) * P],
-                        lhsT=cc[:, t:t + 1].to_broadcast([P, P]),
-                        rhs=ident[:],
-                        start=True,
-                        stop=True,
-                    )
-
-            st_z(e - 4)
-            st_z(o - 4)
-            st_m2(e - 2)
-            if q == 0:
-                st_rt(2)
-                st_rt(3)
-            if q > 0:
-                st_pv(o)
-            st_x(o + 4)
-            if q == 0:
-                st_rx(2)
-                st_rx(3)
-            if q == 1:
+                for m in range(4):
+                    nc.tensor.matmul(out=ccp[:], lhsT=ones[:], rhs=t1[:, :, m], start=(m == 0), stop=(m == 3))
+            if r == 0:
+                st_z(g - 4)
+            if r == 2:
+                st_z(g - 3)
+                st_z(g - 2)
+            st_pv(s)
+            if s == 0:
+                st_cast(0)
+            if s == 1:
+                st_xv(2)
+                st_t(4)
+                st_t(5)
+                st_qx(2)
+                nc.vector.tensor_tensor(out=quad4(ciw), in0=pairs(cB), in1=quad4(iw), op=ALU.mult)
+                nc.gpsimd.tensor_scalar(out=rg[:, 0].rearrange("p r m -> p (r m)"), in0=flat(iw), scalar1=1.0, scalar2=0.0, op0=ALU.mult, op1=ALU.add)
+                nc.gpsimd.tensor_scalar(out=rg[:, 1].rearrange("p r m -> p (r m)"), in0=flat(ciw), scalar1=-2.0, scalar2=0.0, op0=ALU.mult, op1=ALU.add)
+            st_qq(s - 2)
+            if s > 0:
+                st_qx(s + 2)
+            if s == 1:
+                nc.vector.tensor_tensor(out=quad4(t1), in0=pairs(cB), in1=quad4(ciw), op=ALU.mult)
+            if s == 2:
+                nc.vector.quantize_mx(out=rc[:].bitcast(FP8X4), scales=rs[:], in_=rg[:].rearrange("p k r m -> p (k r m)"))
+            st_m2(s - 3)
+            if s > 1:
+                st_cast(s - 1)
+            st_x(s + 3)
+            if r == 0:
+                st_sq(g)
+            if r == 1:
+                st_ps(g + 2)
+                st_sq(g + 1)
+            if r == 2:
+                st_sq(g + 2)
+            if s == 2:
                 nc.scalar.activation(out=ccs[:], in_=ccp[:], func=ACT.Copy, scale=SCALE)
-
-            st_qq(o - 2)
-            st_qx(o + 3)
-            st_cast(o, "G")
-            st_sqs(o)
-            st_sq(o)
-            st_cast(o, "S")
-            st_m1(o + 2)
-            st_m2(o - 2)
+            if s == 1:
+                st_m1(2)
+            if s > 0:
+                st_m1(s + 2)

@@ -188,11 +188,10 @@ def tile_fuzzy_attention_pa_t_kernel(tc, query, Wq, bq, centers, widths, out):
             if not ok(j):
                 return
             dst, src = views(j, 1)
+            if s_pair(j):
+                dst = get_gq(j)[:, 1, :].rearrange("p (t m) -> p t m", m=4)
+                src = qf[j][:].rearrange("p m t -> p t m")
             nc.gpsimd.tensor_scalar(out=dst, in0=src, scalar1=1.0, scalar2=0.0, op0=ALU.mult, op1=ALU.add)
-
-        def st_castv(j):
-            dst, src = views(j, 1)
-            nc.vector.tensor_copy(out=dst, in_=src)
 
         def st_qq(j):
             if not ok(j):

@@ -174,8 +174,8 @@ def tile_fuzzy_attention_pa_t_kernel(tc, query, Wq, bq, centers, widths, out):
 
         def views(j, k):
             if s_pair(j):
-                dst = get_gq(j)[:, k, :].rearrange("p (c i m) -> p c m i", i=4, m=4)
-                return dst, qf[j][:].rearrange("p m (c i) -> p c m i", i=4)
+                dst = get_gq(j)[:, k, :].rearrange("p (t m) -> p t m", m=4)
+                return dst, qf[j][:].rearrange("p m t -> p t m")
             return get_gq(j)[:, k, :], qf[j][:].rearrange("p t m -> p (t m)")
 
         def st_sq(j):
@@ -188,9 +188,6 @@ def tile_fuzzy_attention_pa_t_kernel(tc, query, Wq, bq, centers, widths, out):
             if not ok(j):
                 return
             dst, src = views(j, 1)
-            if s_pair(j):
-                dst = get_gq(j)[:, 1, :].rearrange("p (t m) -> p t m", m=4)
-                src = qf[j][:].rearrange("p m t -> p t m")
             nc.gpsimd.tensor_scalar(out=dst, in0=src, scalar1=1.0, scalar2=0.0, op0=ALU.mult, op1=ALU.add)
 
         def st_qq(j):

@@ -25,7 +25,7 @@ S_FROM = 4
 
 
 def s_pair(j):
-    return j % 3 == 1 and j >= S_FROM
+    return (j + 1) % 5 in [1,3] and j >= S_FROM
 
 
 def tile_fuzzy_attention_pa_t_kernel(tc, query, Wq, bq, centers, widths, out):
@@ -44,14 +44,12 @@ def tile_fuzzy_attention_pa_t_kernel(tc, query, Wq, bq, centers, widths, out):
         bq_sb = const.tile([P, 4], BF16, name="bq_sb")
         w_sb = const.tile([P, 2, D], BF16, name="w_sb")
         c_sb = const.tile([P, 2, D], BF16, name="c_sb")
-        wqv = Wq.rearrange("(c m) i -> c m i", m=4)
-        nc.sync.dma_start(out=wq_sb[:, 0:2, :], in_=wqv[:, 0:2, :])
-        nc.sync.dma_start(out=wq_sb[:, 2:4, :], in_=wqv[:, 2:4, :])
         nc.sync.dma_start(out=x_sb[0][:, 0:2, :], in_=xv[0][:, 0:2, :])
-        nc.sync.dma_start(out=x_sb[0][:, 2:4, :], in_=xv[0][:, 2:4, :])
+        nc.sync.dma_start(out=wq_sb[:], in_=Wq.rearrange("(c m) i -> c m i", m=4))
         nc.sync.dma_start(out=bq_sb[:], in_=bq.rearrange("(c m) -> c m", m=4))
         nc.sync.dma_start(out=w_sb[:], in_=widths.rearrange("(t p) d -> p t d", p=P))
         nc.sync.dma_start(out=c_sb[:], in_=centers.rearrange("(t p) d -> p t d", p=P))
+        nc.sync.dma_start(out=x_sb[0][:, 2:4, :], in_=xv[0][:, 2:4, :])
         for j in range(1, NQUAD):
             nc.sync.dma_start(out=x_sb[j][:], in_=xv[j])
 
@@ -61,9 +59,10 @@ def tile_fuzzy_attention_pa_t_kernel(tc, query, Wq, bq, centers, widths, out):
         nc.scalar.activation(out=warm[:], in_=one[:], func=ACT.Abs_reciprocal_sqrt)
         ident = const.tile([P, P], F32, name="ident")
         make_identity(nc, ident[:])
+        bias = const.tile([P, 4], F32, name="bias")
+        nc.vector.tensor_copy(out=bias[:], in_=bq_sb[:])
         ones = const.tile([P, P], F32, name="ones")
         nc.vector.memset(ones[:], 1.0)
-        bias = const.tile([P, 4], F32, name="bias")
 
         wg = const.tile([P, 2048], BF16, name="wg", align_bytes=64)
         wc = const.tile([P, 512], U32, name="wc", align_bytes=64)
@@ -107,13 +106,6 @@ def tile_fuzzy_attention_pa_t_kernel(tc, query, Wq, bq, centers, widths, out):
                 return
             xg[j] = ring.tile([P, 1024], BF16, name="xg%d" % j, tag="xg", bufs=3, align_bytes=64)
             nc.scalar.copy(
-                out=xg[j][:].bitcast(F32).rearrange("p (a t u) -> p a t u", a=2, u=2),
-                in_=tb[j][:].rearrange("p a u t -> p a t u"),
-            )
-
-        def st_xv(j):
-            xg[j] = ring.tile([P, 1024], BF16, name="xg%d" % j, tag="xg", bufs=3, align_bytes=64)
-            nc.vector.tensor_copy(
                 out=xg[j][:].bitcast(F32).rearrange("p (a t u) -> p a t u", a=2, u=2),
                 in_=tb[j][:].rearrange("p a u t -> p a t u"),
             )
@@ -252,6 +244,8 @@ def tile_fuzzy_attention_pa_t_kernel(tc, query, Wq, bq, centers, widths, out):
         def flat(t):
             return t[:].rearrange("p r m -> p (r m)")
 
+        st_t(0)
+        st_x(0)
         twb = []
         for h in range(2):
             t = psum.tile([P, 2, 2, P], F32, name="twb%d" % h, tag="A", bufs=4)
@@ -260,30 +254,27 @@ def tile_fuzzy_attention_pa_t_kernel(tc, query, Wq, bq, centers, widths, out):
                 words = wq_sb[:, 2 * h + m, :].bitcast(F32)
                 for u in range(2):
                     nc.tensor.transpose(t[:, m, u, :], words[:, u * P:(u + 1) * P], ident[:])
-        st_t(0)
-        st_t(1)
-        wT = rule_t(w_sb, "wT", "Z")
         wgv = wg[:].bitcast(F32).rearrange("p (m c u) -> p m c u", m=4, u=2)
-        nc.vector.tensor_copy(out=wgv[:, 0:2], in_=twb[0][:].rearrange("p m u c -> p m c u"))
-        nc.scalar.copy(out=wgv[:, 2:4], in_=twb[1][:].rearrange("p m u c -> p m c u"))
-        st_x(0)
-        for h in range(2):
-            nc.vector.quantize_mx(out=wc[:, 256 * h:256 * h + 256].bitcast(FP8X4), scales=ws[:, 256 * h:256 * h + 256], in_=wg[:, 1024 * h:1024 * h + 1024])
+        nc.scalar.copy(out=wgv[:, 0:2], in_=twb[0][:].rearrange("p m u c -> p m c u"))
+        nc.vector.tensor_copy(out=wgv[:, 2:4], in_=twb[1][:].rearrange("p m u c -> p m c u"))
         st_qx(0)
-        st_m1(0)
-        nc.vector.tensor_copy(out=bias[:], in_=bq_sb[:])
-        st_x(1)
-        st_qx(1)
+        nc.vector.quantize_mx(out=wc[:].bitcast(FP8X4), scales=ws[:], in_=wg[:])
+        wT = rule_t(w_sb, "wT", "Z")
         nc.scalar.activation(out=quad4(w2), in_=pairs(wT), func=ACT.Square)
-        st_m1(1)
-        st_t(2)
+        st_t(1)
         cB = rule_t(c_sb, "cB", "Z")
-        st_t(3)
+        st_x(1)
         nc.scalar.activation(out=r0[:], in_=w2[:], func=ACT.Abs_reciprocal_sqrt)
         nc.scalar.activation(out=iw[:], in_=r0[:], func=ACT.Square)
+        st_qx(1)
+        st_m1(0)
+        st_t(2)
+        st_t(3)
+        st_x(2)
+        st_m1(1)
 
         for s in range(NPAIR + 5):
-            r = (s + 1) % 3
+            r = (s + 1) % 5
             g = s - r
             if s > 1:
                 st_t(s + 4)
@@ -292,15 +283,17 @@ def tile_fuzzy_attention_pa_t_kernel(tc, query, Wq, bq, centers, widths, out):
                 for m in range(4):
                     nc.tensor.matmul(out=ccp[:], lhsT=ones[:], rhs=t1[:, :, m], start=(m == 0), stop=(m == 3))
             if r == 0:
+                st_z(g - 5)
+            if r == 1:
                 st_z(g - 4)
-            if r == 2:
                 st_z(g - 3)
+            if r == 3:
                 st_z(g - 2)
+                st_z(g - 1)
             st_pv(s)
             if s == 0:
                 st_cast(0)
             if s == 1:
-                st_xv(2)
                 st_t(4)
                 st_t(5)
                 st_qx(2)
@@ -318,13 +311,8 @@ def tile_fuzzy_attention_pa_t_kernel(tc, query, Wq, bq, centers, widths, out):
             if s > 1:
                 st_cast(s - 1)
             st_x(s + 3)
-            if r == 0:
-                st_sq(g)
-            if r == 1:
-                st_ps(g + 2)
-                st_sq(g + 1)
-            if r == 2:
-                st_sq(g + 2)
+            st_ps(s + 1)
+            st_sq(s)
             if s == 2:
                 nc.scalar.activation(out=ccs[:], in_=ccp[:], func=ACT.Copy, scale=SCALE)
             if s == 1:

@@ -15,23 +15,29 @@ P = 128
 TOKENS = 8192
 D = 512
 R = 256
-NQUAD = TOKENS // 512
-NPAIR = TOKENS // 256
+PAIR = 256
+NPAIR = TOKENS // PAIR
+NQUAD = NPAIR // 2
 SCALE = -(0.5 / D)
 FLOPS = 2 * TOKENS * D * D + 2 * 2 * TOKENS * D * R
 
-
-S_FROM = 4
+FIRST_S = 6
+S_COLS = 384
 
 
 def s_pair(j):
-    return (j + 1) % 5 in [1,3] and j >= S_FROM
+    return j >= FIRST_S and j % 3 == 0
+
+
+def z_reads(s):
+    return (2, 0, 1)[s % 3]
 
 
 def tile_fuzzy_attention_pa_t_kernel(tc, query, Wq, bq, centers, widths, out):
     nc = tc.nc
     xv = query.flatten_outer_dims().rearrange("(j p a) i -> j p a i", p=P, a=4)
     ov = out.flatten_outer_dims().rearrange("(j p a) r -> j p a r", p=P, a=4)
+    wqv = Wq.rearrange("(c m) i -> c m i", m=4)
 
     with ExitStack() as ctx:
         ctx.enter_context(tc.manual_schedule())
@@ -44,12 +50,13 @@ def tile_fuzzy_attention_pa_t_kernel(tc, query, Wq, bq, centers, widths, out):
         bq_sb = const.tile([P, 4], BF16, name="bq_sb")
         w_sb = const.tile([P, 2, D], BF16, name="w_sb")
         c_sb = const.tile([P, 2, D], BF16, name="c_sb")
+        nc.sync.dma_start(out=wq_sb[:, 0:2, :], in_=wqv[:, 0:2, :])
+        nc.sync.dma_start(out=wq_sb[:, 2:4, :], in_=wqv[:, 2:4, :])
         nc.sync.dma_start(out=x_sb[0][:, 0:2, :], in_=xv[0][:, 0:2, :])
-        nc.sync.dma_start(out=wq_sb[:], in_=Wq.rearrange("(c m) i -> c m i", m=4))
         nc.sync.dma_start(out=bq_sb[:], in_=bq.rearrange("(c m) -> c m", m=4))
+        nc.sync.dma_start(out=x_sb[0][:, 2:4, :], in_=xv[0][:, 2:4, :])
         nc.sync.dma_start(out=w_sb[:], in_=widths.rearrange("(t p) d -> p t d", p=P))
         nc.sync.dma_start(out=c_sb[:], in_=centers.rearrange("(t p) d -> p t d", p=P))
-        nc.sync.dma_start(out=x_sb[0][:, 2:4, :], in_=xv[0][:, 2:4, :])
         for j in range(1, NQUAD):
             nc.sync.dma_start(out=x_sb[j][:], in_=xv[j])
 
@@ -59,10 +66,9 @@ def tile_fuzzy_attention_pa_t_kernel(tc, query, Wq, bq, centers, widths, out):
         nc.scalar.activation(out=warm[:], in_=one[:], func=ACT.Abs_reciprocal_sqrt)
         ident = const.tile([P, P], F32, name="ident")
         make_identity(nc, ident[:])
-        bias = const.tile([P, 4], F32, name="bias")
-        nc.vector.tensor_copy(out=bias[:], in_=bq_sb[:])
         ones = const.tile([P, P], F32, name="ones")
         nc.vector.memset(ones[:], 1.0)
+        bias = const.tile([P, 4], F32, name="bias")
 
         wg = const.tile([P, 2048], BF16, name="wg", align_bytes=64)
         wc = const.tile([P, 512], U32, name="wc", align_bytes=64)
@@ -78,22 +84,16 @@ def tile_fuzzy_attention_pa_t_kernel(tc, query, Wq, bq, centers, widths, out):
         rs = const.tile([P, 512], U8, name="rs", align_bytes=64)
         zs = [const.tile([P, 4, R], F32, name="zs%d" % j) for j in range(NQUAD)]
 
-        tb = {}
-        xg = {}
-        xc = {}
-        xs = {}
-        ab = {}
-        qf = {}
-        gq = {}
-        qc = {}
-        qs = {}
-        zb = {}
+        tb, xg, xc, xs, ab, qf, gq, qc, qs, zb = {}, {}, {}, {}, {}, {}, {}, {}, {}, {}
 
-        def ok(j):
+        def real(j):
             return 0 <= j < NPAIR
 
-        def st_t(j):
-            if not ok(j):
+        def gcast(dst, src, factor):
+            nc.gpsimd.tensor_scalar(out=dst, in0=src, scalar1=factor, scalar2=0.0, op0=ALU.mult, op1=ALU.add)
+
+        def transpose_x(j):
+            if not real(j):
                 return
             tb[j] = psum.tile([P, 2, 2, P], F32, name="tb%d" % j, tag="T", bufs=2)
             for a in range(2):
@@ -101,47 +101,47 @@ def tile_fuzzy_attention_pa_t_kernel(tc, query, Wq, bq, centers, widths, out):
                 for u in range(2):
                     nc.tensor.transpose(tb[j][:, a, u, :], words[:, u * P:(u + 1) * P], ident[:])
 
-        def st_x(j):
-            if not ok(j):
+        def copy_x(j, copy):
+            if not real(j):
                 return
             xg[j] = ring.tile([P, 1024], BF16, name="xg%d" % j, tag="xg", bufs=3, align_bytes=64)
-            nc.scalar.copy(
+            copy(
                 out=xg[j][:].bitcast(F32).rearrange("p (a t u) -> p a t u", a=2, u=2),
                 in_=tb[j][:].rearrange("p a u t -> p a t u"),
             )
 
-        def st_qx(j):
-            if not ok(j):
+        def quantise_x(j):
+            if not real(j):
                 return
-            xc[j] = ring.tile([P, 256], U32, name="xc%d" % j, tag="xc", bufs=4, align_bytes=64)
-            xs[j] = ring.tile([P, 256], U8, name="xs%d" % j, tag="xs", bufs=4, align_bytes=64)
+            xc[j] = ring.tile([P, PAIR], U32, name="xc%d" % j, tag="xc", bufs=4, align_bytes=64)
+            xs[j] = ring.tile([P, PAIR], U8, name="xs%d" % j, tag="xs", bufs=4, align_bytes=64)
             nc.vector.quantize_mx(out=xc[j][:].bitcast(FP8X4), scales=xs[j][:], in_=xg[j][:])
 
-        def st_m1(j):
-            if not ok(j):
+        def project(j):
+            if not real(j):
                 return
-            wide = 256 if s_pair(j) else P
-            per = 512 // wide
+            width = PAIR if s_pair(j) else P
+            groups = 512 // width
             for h in range(2):
-                acc = psum.tile([P, per, wide], F32, name="ab%d_%d" % (j, h), tag="A", bufs=4)
+                acc = psum.tile([P, groups, width], F32, name="ab%d_%d" % (j, h), tag="A", bufs=4)
                 ab[(j, h)] = acc
-                for n in range(per):
+                for n in range(groups):
                     m = 2 * h + n if s_pair(j) else n
                     lo = 0 if s_pair(j) else h * P
                     nc.tensor.matmul_mx(
                         out=acc[:, n, :],
                         lhsT=wc[:, m * P:(m + 1) * P].bitcast(FP8X4),
                         lhsT_scale=ws[:, m * P:(m + 1) * P],
-                        rhs=xc[j][:, lo:lo + wide].bitcast(FP8X4),
-                        rhs_scale=xs[j][:, lo:lo + wide],
+                        rhs=xc[j][:, lo:lo + width].bitcast(FP8X4),
+                        rhs_scale=xs[j][:, lo:lo + width],
                         start=True,
                         stop=True,
                     )
 
-        def st_pv(j):
-            if not ok(j) or s_pair(j):
+        def bias_on_vector(j):
+            if not real(j) or s_pair(j):
                 return
-            qf[j] = ring.tile([P, 256, 4], F32, name="qf%d" % j, tag="qf", bufs=3)
+            qf[j] = ring.tile([P, PAIR, 4], F32, name="qf%d" % j, tag="qf", bufs=3)
             for a in range(2):
                 nc.vector.tensor_tensor(
                     out=qf[j][:, a * P:(a + 1) * P, :],
@@ -150,40 +150,53 @@ def tile_fuzzy_attention_pa_t_kernel(tc, query, Wq, bq, centers, widths, out):
                     op=ALU.add,
                 )
 
-        def st_ps(j):
-            if not ok(j) or not s_pair(j):
+        def bias_on_scalar(j):
+            if not real(j) or not s_pair(j):
                 return
-            qf[j] = ring.tile([P, 4, 256], F32, name="qp%d" % j, tag="qp", bufs=2)
+            qf[j] = ring.tile([P, 4, PAIR], F32, name="qp%d" % j, tag="qp", bufs=2)
             for m in range(4):
                 nc.scalar.activation(
                     out=qf[j][:, m, :], in_=ab[(j, m // 2)][:, m % 2, :], func=ACT.Identity, bias=bias[:, m:m + 1]
                 )
 
-        def get_gq(j):
+        def grouped(j):
             if j not in gq:
-                gq[j] = ring.tile([P, 2, 1024], BF16, name="gq%d" % j, tag="gq", bufs=2, align_bytes=64)
+                own = j >= NPAIR - 2
+                gq[j] = ring.tile(
+                    [P, 2, 1024],
+                    BF16,
+                    name="gq%d" % j,
+                    tag="gl%d" % j if own else "gq",
+                    bufs=1 if own else 2,
+                    align_bytes=64,
+                )
             return gq[j]
 
-        def views(j, k):
+        def views(j, k, lo, hi):
+            dst = grouped(j)[:, k, lo:hi]
             if s_pair(j):
-                dst = get_gq(j)[:, k, :].rearrange("p (t m) -> p t m", m=4)
-                return dst, qf[j][:].rearrange("p m t -> p t m")
-            return get_gq(j)[:, k, :], qf[j][:].rearrange("p t m -> p (t m)")
+                return dst.rearrange("p (t m) -> p t m", m=4), qf[j][:].rearrange("p m t -> p t m")[:, lo // 4:hi // 4, :]
+            return dst, qf[j][:].rearrange("p t m -> p (t m)")[:, lo:hi]
 
-        def st_sq(j):
-            if not ok(j):
+        def square(j):
+            if not real(j):
                 return
-            dst, src = views(j, 0)
+            dst, src = views(j, 0, 0, 1024)
             nc.scalar.activation(out=dst, in_=src, func=ACT.Square)
 
-        def st_cast(j):
-            if not ok(j):
+        def round_on_gpsimd(j):
+            if not real(j):
                 return
-            dst, src = views(j, 1)
-            nc.gpsimd.tensor_scalar(out=dst, in0=src, scalar1=1.0, scalar2=0.0, op0=ALU.mult, op1=ALU.add)
+            gcast(*views(j, 1, S_COLS if s_pair(j) else 0, 1024), 1.0)
 
-        def st_qq(j):
-            if not ok(j):
+        def round_on_scalar(j):
+            if not real(j) or not s_pair(j):
+                return
+            dst, src = views(j, 1, 0, S_COLS)
+            nc.scalar.copy(out=dst, in_=src)
+
+        def quantise_q(j):
+            if not real(j):
                 return
             qc[j] = ring.tile([P, 512], U32, name="qc%d" % j, tag="qc", bufs=4, align_bytes=64)
             qs[j] = ring.tile([P, 512], U8, name="qs%d" % j, tag="qs", bufs=4, align_bytes=64)
@@ -193,13 +206,13 @@ def tile_fuzzy_attention_pa_t_kernel(tc, query, Wq, bq, centers, widths, out):
                 in_=gq[j][:].rearrange("p k c -> p (k c)"),
             )
 
-        def st_m2(j):
-            if not ok(j):
+        def rules(j):
+            if not real(j):
                 return
             zb[j] = psum.tile([P, 2, R], F32, name="zb%d" % j, tag="Z", bufs=2)
             for a in range(2):
                 for k in range(2):
-                    lo = k * 256 + a * P
+                    lo = k * PAIR + a * P
                     nc.tensor.matmul_mx(
                         out=zb[j][:, a, :],
                         lhsT=qc[j][:, lo:lo + P].bitcast(FP8X4),
@@ -210,112 +223,118 @@ def tile_fuzzy_attention_pa_t_kernel(tc, query, Wq, bq, centers, widths, out):
                         stop=(k == 1),
                     )
 
-        def st_z(j):
-            if not ok(j):
-                return
+        def finish(j):
             h = 2 * (j % 2)
+            z = zs[j // 2]
+            if j == NPAIR - 1:
+                for a in range(2):
+                    nc.vector.scalar_tensor_tensor(
+                        out=z[:, h + a, :], in0=zb[j][:, a, :], scalar=SCALE, in1=ccs[:], op0=ALU.mult, op1=ALU.add
+                    )
+                    nc.sync.dma_start(out=ov[j // 2][:, h + a, :], in_=z[:, h + a, :])
+                return
             nc.vector.scalar_tensor_tensor(
-                out=zs[j // 2][:, h:h + 2, :],
+                out=z[:, h:h + 2, :],
                 in0=zb[j][:],
                 scalar=SCALE,
                 in1=ccs[:].unsqueeze(1).to_broadcast([P, 2, R]),
                 op0=ALU.mult,
                 op1=ALU.add,
             )
-            if j >= NPAIR - 2:
-                nc.sync.dma_start(out=ov[j // 2][:, h:h + 2, :], in_=zs[j // 2][:, h:h + 2, :])
+            if j == NPAIR - 2:
+                nc.sync.dma_start(out=ov[j // 2][:, h:h + 2, :], in_=z[:, h:h + 2, :])
             elif j % 2 == 1:
-                nc.sync.dma_start(out=ov[j // 2], in_=zs[j // 2][:])
+                nc.sync.dma_start(out=ov[j // 2], in_=z[:])
 
-        def rule_t(src, name, tag):
-            bank = psum.tile([P, 2, R], F32, name=name, tag=tag, bufs=4 if tag == "A" else 2)
+        def transpose_rules(src, name):
+            bank = psum.tile([P, 2, R], F32, name=name, tag="Z", bufs=2)
             for t in range(2):
                 words = src[:, t, :].bitcast(F32)
                 for u in range(2):
                     nc.tensor.transpose(bank[:, u, t * P:(t + 1) * P], words[:, u:2 * P:2], ident[:])
             return bank
 
-        def pairs(bank):
+        def bank_values(bank):
             return bank[:].rearrange("p u r -> p (u r)").bitcast(BF16).rearrange("p (u r e) -> p r u e", u=2, e=2)
 
-        def quad4(t):
+        def by_word(t):
             return t[:].rearrange("p r (u e) -> p r u e", u=2)
 
         def flat(t):
-            return t[:].rearrange("p r m -> p (r m)")
+            return t.rearrange("p r m -> p (r m)")
 
-        st_t(0)
-        st_x(0)
         twb = []
         for h in range(2):
-            t = psum.tile([P, 2, 2, P], F32, name="twb%d" % h, tag="A", bufs=4)
-            twb.append(t)
+            bank = psum.tile([P, 2, 2, P], F32, name="twb%d" % h, tag="A", bufs=4)
+            twb.append(bank)
             for m in range(2):
                 words = wq_sb[:, 2 * h + m, :].bitcast(F32)
                 for u in range(2):
-                    nc.tensor.transpose(t[:, m, u, :], words[:, u * P:(u + 1) * P], ident[:])
+                    nc.tensor.transpose(bank[:, m, u, :], words[:, u * P:(u + 1) * P], ident[:])
+        transpose_x(0)
+        transpose_x(1)
+        w_bank = transpose_rules(w_sb, "w_bank")
         wgv = wg[:].bitcast(F32).rearrange("p (m c u) -> p m c u", m=4, u=2)
-        nc.scalar.copy(out=wgv[:, 0:2], in_=twb[0][:].rearrange("p m u c -> p m c u"))
-        nc.vector.tensor_copy(out=wgv[:, 2:4], in_=twb[1][:].rearrange("p m u c -> p m c u"))
-        st_qx(0)
-        nc.vector.quantize_mx(out=wc[:].bitcast(FP8X4), scales=ws[:], in_=wg[:])
-        wT = rule_t(w_sb, "wT", "Z")
-        nc.scalar.activation(out=quad4(w2), in_=pairs(wT), func=ACT.Square)
-        st_t(1)
-        cB = rule_t(c_sb, "cB", "Z")
-        st_x(1)
+        nc.vector.tensor_copy(out=wgv[:, 0:2], in_=twb[0][:].rearrange("p m u c -> p m c u"))
+        nc.scalar.copy(out=wgv[:, 2:4], in_=twb[1][:].rearrange("p m u c -> p m c u"))
+        copy_x(0, nc.scalar.copy)
+        for h in range(2):
+            nc.vector.quantize_mx(
+                out=wc[:, 256 * h:256 * h + 256].bitcast(FP8X4),
+                scales=ws[:, 256 * h:256 * h + 256],
+                in_=wg[:, 1024 * h:1024 * h + 1024],
+            )
+        quantise_x(0)
+        project(0)
+        nc.vector.tensor_copy(out=bias[:], in_=bq_sb[:])
+        copy_x(1, nc.scalar.copy)
+        quantise_x(1)
+        nc.scalar.activation(out=by_word(w2), in_=bank_values(w_bank), func=ACT.Square)
+        project(1)
+        transpose_x(2)
+        c_bank = transpose_rules(c_sb, "c_bank")
+        transpose_x(3)
         nc.scalar.activation(out=r0[:], in_=w2[:], func=ACT.Abs_reciprocal_sqrt)
         nc.scalar.activation(out=iw[:], in_=r0[:], func=ACT.Square)
-        st_qx(1)
-        st_m1(0)
-        st_t(2)
-        st_t(3)
-        st_x(2)
-        st_m1(1)
 
-        for s in range(NPAIR + 5):
-            r = (s + 1) % 5
-            g = s - r
+        z_next = 0
+        for s in range(NPAIR + 6):
             if s > 1:
-                st_t(s + 4)
-            if s == 2:
-                ccp = psum.tile([P, R], F32, name="ccp", tag="Z", bufs=2)
-                for m in range(4):
-                    nc.tensor.matmul(out=ccp[:], lhsT=ones[:], rhs=t1[:, :, m], start=(m == 0), stop=(m == 3))
-            if r == 0:
-                st_z(g - 5)
-            if r == 1:
-                st_z(g - 4)
-                st_z(g - 3)
-            if r == 3:
-                st_z(g - 2)
-                st_z(g - 1)
-            st_pv(s)
+                transpose_x(s + 4)
+            for n in range(z_reads(s) if s <= NPAIR else 2):
+                if z_next < NPAIR and z_next <= s - 4:
+                    finish(z_next)
+                    z_next += 1
+            bias_on_vector(s)
             if s == 0:
-                st_cast(0)
+                round_on_gpsimd(0)
             if s == 1:
-                st_t(4)
-                st_t(5)
-                st_qx(2)
-                nc.vector.tensor_tensor(out=quad4(ciw), in0=pairs(cB), in1=quad4(iw), op=ALU.mult)
-                nc.gpsimd.tensor_scalar(out=rg[:, 0].rearrange("p r m -> p (r m)"), in0=flat(iw), scalar1=1.0, scalar2=0.0, op0=ALU.mult, op1=ALU.add)
-                nc.gpsimd.tensor_scalar(out=rg[:, 1].rearrange("p r m -> p (r m)"), in0=flat(ciw), scalar1=-2.0, scalar2=0.0, op0=ALU.mult, op1=ALU.add)
-            st_qq(s - 2)
+                copy_x(2, nc.vector.tensor_copy)
+                transpose_x(4)
+                transpose_x(5)
+                quantise_x(2)
+                nc.vector.tensor_tensor(out=by_word(ciw), in0=bank_values(c_bank), in1=by_word(iw), op=ALU.mult)
+                gcast(flat(rg[:, 0]), flat(iw[:]), 1.0)
+                gcast(flat(rg[:, 1]), flat(ciw[:]), -2.0)
+            quantise_q(s - 2)
             if s > 0:
-                st_qx(s + 2)
+                quantise_x(s + 2)
             if s == 1:
-                nc.vector.tensor_tensor(out=quad4(t1), in0=pairs(cB), in1=quad4(ciw), op=ALU.mult)
+                nc.vector.tensor_tensor(out=by_word(t1), in0=bank_values(c_bank), in1=by_word(ciw), op=ALU.mult)
             if s == 2:
                 nc.vector.quantize_mx(out=rc[:].bitcast(FP8X4), scales=rs[:], in_=rg[:].rearrange("p k r m -> p (k r m)"))
-            st_m2(s - 3)
+                cc_bank = psum.tile([P, R], F32, name="cc_bank", tag="Z", bufs=2)
+                for m in range(4):
+                    nc.tensor.matmul(out=cc_bank[:], lhsT=ones[:], rhs=t1[:, :, m], start=(m == 0), stop=(m == 3))
+                nc.scalar.activation(out=ccs[:], in_=cc_bank[:], func=ACT.Copy, scale=SCALE)
+            rules(s - 3)
             if s > 1:
-                st_cast(s - 1)
-            st_x(s + 3)
-            st_ps(s + 1)
-            st_sq(s)
-            if s == 2:
-                nc.scalar.activation(out=ccs[:], in_=ccp[:], func=ACT.Copy, scale=SCALE)
+                round_on_gpsimd(s - 1)
+            copy_x(s + 3, nc.scalar.copy)
+            bias_on_scalar(s + 1)
+            square(s)
+            round_on_scalar(s)
             if s == 1:
-                st_m1(2)
+                project(2)
             if s > 0:
-                st_m1(s + 2)
+                project(s + 2)

@@ -153,7 +153,8 @@ def tile_fuzzy_attention_pa_t_kernel(tc, query, Wq, bq, centers, widths, out):
         def bias_on_scalar(j):
             if not real(j) or not s_pair(j):
                 return
-            qf[j] = ring.tile([P, 4, PAIR], F32, name="qp%d" % j, tag="qp", bufs=2)
+            full = ring.tile([P, 4, PAIR + 4], F32, name="qp%d" % j, tag="qp", bufs=2)
+            qf[j] = full[:, :, 0:PAIR]
             for m in range(4):
                 nc.scalar.activation(
                     out=qf[j][:, m, :], in_=ab[(j, m // 2)][:, m % 2, :], func=ACT.Identity, bias=bias[:, m:m + 1]
@@ -161,7 +162,7 @@ def tile_fuzzy_attention_pa_t_kernel(tc, query, Wq, bq, centers, widths, out):
 
         def grouped(j):
             if j not in gq:
-                own = j >= NPAIR - 2
+                own = j >= NPAIR - 1
                 gq[j] = ring.tile(
                     [P, 2, 1024],
                     BF16,
@@ -175,7 +176,7 @@ def tile_fuzzy_attention_pa_t_kernel(tc, query, Wq, bq, centers, widths, out):
         def views(j, k, lo, hi):
             dst = grouped(j)[:, k, lo:hi]
             if s_pair(j):
-                return dst.rearrange("p (t m) -> p t m", m=4), qf[j][:].rearrange("p m t -> p t m")[:, lo // 4:hi // 4, :]
+                return dst.rearrange("p (t m) -> p t m", m=4), qf[j].rearrange("p m t -> p t m")[:, lo // 4:hi // 4, :]
             return dst, qf[j][:].rearrange("p t m -> p (t m)")[:, lo:hi]
 
         def square(j):

from contextlib import ExitStack

import concourse.mybir as mybir
from concourse.masks import make_identity

F32 = mybir.dt.float32
BF16 = mybir.dt.bfloat16
U32 = mybir.dt.uint32
U8 = mybir.dt.uint8
FP8X4 = mybir.dt.float8_e4m3fn_x4
ALU = mybir.AluOpType
ACT = mybir.ActivationFunctionType

P = 128
TOKENS = 8192
D = 512
R = 256
PAIR = 256
NPAIR = TOKENS // PAIR
NQUAD = NPAIR // 2
SCALE = -(0.5 / D)
FLOPS = 2 * TOKENS * D * D + 2 * 2 * TOKENS * D * R

FIRST_S = 6
S_COLS = 384


def s_pair(j):
    return j >= FIRST_S and j % 3 == 0


def z_reads(s):
    return (2, 0, 1)[s % 3]


def tile_fuzzy_attention_pa_t_kernel(tc, query, Wq, bq, centers, widths, out):
    nc = tc.nc
    xv = query.flatten_outer_dims().rearrange("(j p a) i -> j p a i", p=P, a=4)
    ov = out.flatten_outer_dims().rearrange("(j p a) r -> j p a r", p=P, a=4)
    wqv = Wq.rearrange("(c m) i -> c m i", m=4)

    with ExitStack() as ctx:
        ctx.enter_context(tc.manual_schedule())
        const = ctx.enter_context(tc.tile_pool(name="const", bufs=1))
        ring = ctx.enter_context(tc.tile_pool(name="ring", bufs=4))
        psum = ctx.enter_context(tc.psum_pool(name="psum", bufs=2))

        x_sb = [const.tile([P, 4, D], BF16, name="x%d" % j) for j in range(NQUAD)]
        wq_sb = const.tile([P, 4, D], BF16, name="wq_sb")
        bq_sb = const.tile([P, 4], BF16, name="bq_sb")
        w_sb = const.tile([P, 2, D], BF16, name="w_sb")
        c_sb = const.tile([P, 2, D], BF16, name="c_sb")
        nc.sync.dma_start(out=wq_sb[:, 0:2, :], in_=wqv[:, 0:2, :])
        nc.sync.dma_start(out=wq_sb[:, 2:4, :], in_=wqv[:, 2:4, :])
        nc.sync.dma_start(out=x_sb[0][:, 0:2, :], in_=xv[0][:, 0:2, :])
        nc.sync.dma_start(out=bq_sb[:], in_=bq.rearrange("(c m) -> c m", m=4))
        nc.sync.dma_start(out=x_sb[0][:, 2:4, :], in_=xv[0][:, 2:4, :])
        nc.sync.dma_start(out=w_sb[:], in_=widths.rearrange("(t p) d -> p t d", p=P))
        nc.sync.dma_start(out=c_sb[:], in_=centers.rearrange("(t p) d -> p t d", p=P))
        for j in range(1, NQUAD):
            nc.sync.dma_start(out=x_sb[j][:], in_=xv[j])

        one = const.tile([P, 1], F32, name="one")
        warm = const.tile([P, 1], F32, name="warm")
        nc.vector.memset(one[:], 1.0)
        nc.scalar.activation(out=warm[:], in_=one[:], func=ACT.Abs_reciprocal_sqrt)
        ident = const.tile([P, P], F32, name="ident")
        make_identity(nc, ident[:])
        ones = const.tile([P, P], F32, name="ones")
        nc.vector.memset(ones[:], 1.0)
        bias = const.tile([P, 4], F32, name="bias")

        wg = const.tile([P, 2048], BF16, name="wg", align_bytes=64)
        wc = const.tile([P, 512], U32, name="wc", align_bytes=64)
        ws = const.tile([P, 512], U8, name="ws", align_bytes=64)
        w2 = const.tile([P, R, 4], F32, name="w2")
        r0 = const.tile([P, R, 4], F32, name="r0")
        iw = const.tile([P, R, 4], F32, name="iw")
        ciw = const.tile([P, R, 4], F32, name="ciw")
        t1 = const.tile([P, R, 4], F32, name="t1")
        ccs = const.tile([P, R], F32, name="ccs")
        rg = const.tile([P, 2, R, 4], BF16, name="rg", align_bytes=64)
        rc = const.tile([P, 512], U32, name="rc", align_bytes=64)
        rs = const.tile([P, 512], U8, name="rs", align_bytes=64)
        zs = [const.tile([P, 4, R], F32, name="zs%d" % j) for j in range(NQUAD)]

        tb, xg, xc, xs, ab, qf, gq, qc, qs, zb = {}, {}, {}, {}, {}, {}, {}, {}, {}, {}

        def real(j):
            return 0 <= j < NPAIR

        def gcast(dst, src, factor):
            nc.gpsimd.tensor_scalar(out=dst, in0=src, scalar1=factor, scalar2=0.0, op0=ALU.mult, op1=ALU.add)

        def transpose_x(j):
            if not real(j):
                return
            tb[j] = psum.tile([P, 2, 2, P], F32, name="tb%d" % j, tag="T", bufs=2)
            for a in range(2):
                words = x_sb[j // 2][:, 2 * (j % 2) + a, :].bitcast(F32)
                for u in range(2):
                    nc.tensor.transpose(tb[j][:, a, u, :], words[:, u * P:(u + 1) * P], ident[:])

        def copy_x(j, copy):
            if not real(j):
                return
            xg[j] = ring.tile([P, 1024], BF16, name="xg%d" % j, tag="xg", bufs=3, align_bytes=64)
            copy(
                out=xg[j][:].bitcast(F32).rearrange("p (a t u) -> p a t u", a=2, u=2),
                in_=tb[j][:].rearrange("p a u t -> p a t u"),
            )

        def quantise_x(j):
            if not real(j):
                return
            xc[j] = ring.tile([P, PAIR], U32, name="xc%d" % j, tag="xc", bufs=4, align_bytes=64)
            xs[j] = ring.tile([P, PAIR], U8, name="xs%d" % j, tag="xs", bufs=4, align_bytes=64)
            nc.vector.quantize_mx(out=xc[j][:].bitcast(FP8X4), scales=xs[j][:], in_=xg[j][:])

        def project(j):
            if not real(j):
                return
            width = PAIR if s_pair(j) else P
            groups = 512 // width
            for h in range(2):
                acc = psum.tile([P, groups, width], F32, name="ab%d_%d" % (j, h), tag="A", bufs=4)
                ab[(j, h)] = acc
                for n in range(groups):
                    m = 2 * h + n if s_pair(j) else n
                    lo = 0 if s_pair(j) else h * P
                    nc.tensor.matmul_mx(
                        out=acc[:, n, :],
                        lhsT=wc[:, m * P:(m + 1) * P].bitcast(FP8X4),
                        lhsT_scale=ws[:, m * P:(m + 1) * P],
                        rhs=xc[j][:, lo:lo + width].bitcast(FP8X4),
                        rhs_scale=xs[j][:, lo:lo + width],
                        start=True,
                        stop=True,
                    )

        def bias_on_vector(j):
            if not real(j) or s_pair(j):
                return
            qf[j] = ring.tile([P, PAIR, 4], F32, name="qf%d" % j, tag="qf", bufs=3)
            for a in range(2):
                nc.vector.tensor_tensor(
                    out=qf[j][:, a * P:(a + 1) * P, :],
                    in0=ab[(j, a)][:].rearrange("p m t -> p t m"),
                    in1=bias[:].unsqueeze(1).to_broadcast([P, P, 4]),
                    op=ALU.add,
                )

        def bias_on_scalar(j):
            if not real(j) or not s_pair(j):
                return
            full = ring.tile([P, 4, PAIR + 4], F32, name="qp%d" % j, tag="qp", bufs=2)
            qf[j] = full[:, :, 0:PAIR]
            for m in range(4):
                nc.scalar.activation(
                    out=qf[j][:, m, :], in_=ab[(j, m // 2)][:, m % 2, :], func=ACT.Identity, bias=bias[:, m:m + 1]
                )

        def grouped(j):
            if j not in gq:
                own = j >= NPAIR - 1
                gq[j] = ring.tile(
                    [P, 2, 1024],
                    BF16,
                    name="gq%d" % j,
                    tag="gl%d" % j if own else "gq",
                    bufs=1 if own else 2,
                    align_bytes=64,
                )
            return gq[j]

        def views(j, k, lo, hi):
            dst = grouped(j)[:, k, lo:hi]
            if s_pair(j):
                return dst.rearrange("p (t m) -> p t m", m=4), qf[j].rearrange("p m t -> p t m")[:, lo // 4:hi // 4, :]
            return dst, qf[j][:].rearrange("p t m -> p (t m)")[:, lo:hi]

        def square(j):
            if not real(j):
                return
            dst, src = views(j, 0, 0, 1024)
            nc.scalar.activation(out=dst, in_=src, func=ACT.Square)

        def round_on_gpsimd(j):
            if not real(j):
                return
            gcast(*views(j, 1, S_COLS if s_pair(j) else 0, 1024), 1.0)

        def round_on_scalar(j):
            if not real(j) or not s_pair(j):
                return
            dst, src = views(j, 1, 0, S_COLS)
            nc.scalar.copy(out=dst, in_=src)

        def quantise_q(j):
            if not real(j):
                return
            qc[j] = ring.tile([P, 512], U32, name="qc%d" % j, tag="qc", bufs=4, align_bytes=64)
            qs[j] = ring.tile([P, 512], U8, name="qs%d" % j, tag="qs", bufs=4, align_bytes=64)
            nc.vector.quantize_mx(
                out=qc[j][:].bitcast(FP8X4),
                scales=qs[j][:],
                in_=gq[j][:].rearrange("p k c -> p (k c)"),
            )

        def rules(j):
            if not real(j):
                return
            zb[j] = psum.tile([P, 2, R], F32, name="zb%d" % j, tag="Z", bufs=2)
            for a in range(2):
                for k in range(2):
                    lo = k * PAIR + a * P
                    nc.tensor.matmul_mx(
                        out=zb[j][:, a, :],
                        lhsT=qc[j][:, lo:lo + P].bitcast(FP8X4),
                        lhsT_scale=qs[j][:, lo:lo + P],
                        rhs=rc[:, k * R:(k + 1) * R].bitcast(FP8X4),
                        rhs_scale=rs[:, k * R:(k + 1) * R],
                        start=(k == 0),
                        stop=(k == 1),
                    )

        def finish(j):
            h = 2 * (j % 2)
            z = zs[j // 2]
            if j == NPAIR - 1:
                for a in range(2):
                    nc.vector.scalar_tensor_tensor(
                        out=z[:, h + a, :], in0=zb[j][:, a, :], scalar=SCALE, in1=ccs[:], op0=ALU.mult, op1=ALU.add
                    )
                    nc.sync.dma_start(out=ov[j // 2][:, h + a, :], in_=z[:, h + a, :])
                return
            nc.vector.scalar_tensor_tensor(
                out=z[:, h:h + 2, :],
                in0=zb[j][:],
                scalar=SCALE,
                in1=ccs[:].unsqueeze(1).to_broadcast([P, 2, R]),
                op0=ALU.mult,
                op1=ALU.add,
            )
            if j == NPAIR - 2:
                nc.sync.dma_start(out=ov[j // 2][:, h:h + 2, :], in_=z[:, h:h + 2, :])
            elif j % 2 == 1:
                nc.sync.dma_start(out=ov[j // 2], in_=z[:])

        def transpose_rules(src, name):
            bank = psum.tile([P, 2, R], F32, name=name, tag="Z", bufs=2)
            for t in range(2):
                words = src[:, t, :].bitcast(F32)
                for u in range(2):
                    nc.tensor.transpose(bank[:, u, t * P:(t + 1) * P], words[:, u:2 * P:2], ident[:])
            return bank

        def bank_values(bank):
            return bank[:].rearrange("p u r -> p (u r)").bitcast(BF16).rearrange("p (u r e) -> p r u e", u=2, e=2)

        def by_word(t):
            return t[:].rearrange("p r (u e) -> p r u e", u=2)

        def flat(t):
            return t.rearrange("p r m -> p (r m)")

        twb = []
        for h in range(2):
            bank = psum.tile([P, 2, 2, P], F32, name="twb%d" % h, tag="A", bufs=4)
            twb.append(bank)
            for m in range(2):
                words = wq_sb[:, 2 * h + m, :].bitcast(F32)
                for u in range(2):
                    nc.tensor.transpose(bank[:, m, u, :], words[:, u * P:(u + 1) * P], ident[:])
        transpose_x(0)
        transpose_x(1)
        w_bank = transpose_rules(w_sb, "w_bank")
        wgv = wg[:].bitcast(F32).rearrange("p (m c u) -> p m c u", m=4, u=2)
        nc.vector.tensor_copy(out=wgv[:, 0:2], in_=twb[0][:].rearrange("p m u c -> p m c u"))
        nc.scalar.copy(out=wgv[:, 2:4], in_=twb[1][:].rearrange("p m u c -> p m c u"))
        copy_x(0, nc.scalar.copy)
        for h in range(2):
            nc.vector.quantize_mx(
                out=wc[:, 256 * h:256 * h + 256].bitcast(FP8X4),
                scales=ws[:, 256 * h:256 * h + 256],
                in_=wg[:, 1024 * h:1024 * h + 1024],
            )
        quantise_x(0)
        project(0)
        nc.vector.tensor_copy(out=bias[:], in_=bq_sb[:])
        copy_x(1, nc.scalar.copy)
        quantise_x(1)
        nc.scalar.activation(out=by_word(w2), in_=bank_values(w_bank), func=ACT.Square)
        project(1)
        transpose_x(2)
        c_bank = transpose_rules(c_sb, "c_bank")
        transpose_x(3)
        nc.scalar.activation(out=r0[:], in_=w2[:], func=ACT.Abs_reciprocal_sqrt)
        nc.scalar.activation(out=iw[:], in_=r0[:], func=ACT.Square)

        z_next = 0
        for s in range(NPAIR + 6):
            if s > 1:
                transpose_x(s + 4)
            for n in range(z_reads(s) if s <= NPAIR else 2):
                if z_next < NPAIR and z_next <= s - 4:
                    finish(z_next)
                    z_next += 1
            bias_on_vector(s)
            if s == 0:
                round_on_gpsimd(0)
            if s == 1:
                copy_x(2, nc.vector.tensor_copy)
                transpose_x(4)
                transpose_x(5)
                quantise_x(2)
                nc.vector.tensor_tensor(out=by_word(ciw), in0=bank_values(c_bank), in1=by_word(iw), op=ALU.mult)
                gcast(flat(rg[:, 0]), flat(iw[:]), 1.0)
                gcast(flat(rg[:, 1]), flat(ciw[:]), -2.0)
            quantise_q(s - 2)
            if s > 0:
                quantise_x(s + 2)
            if s == 1:
                nc.vector.tensor_tensor(out=by_word(t1), in0=bank_values(c_bank), in1=by_word(ciw), op=ALU.mult)
            if s == 2:
                nc.vector.quantize_mx(out=rc[:].bitcast(FP8X4), scales=rs[:], in_=rg[:].rearrange("p k r m -> p (k r m)"))
                cc_bank = psum.tile([P, R], F32, name="cc_bank", tag="Z", bufs=2)
                for m in range(4):
                    nc.tensor.matmul(out=cc_bank[:], lhsT=ones[:], rhs=t1[:, :, m], start=(m == 0), stop=(m == 3))
                nc.scalar.activation(out=ccs[:], in_=cc_bank[:], func=ACT.Copy, scale=SCALE)
            rules(s - 3)
            if s > 1:
                round_on_gpsimd(s - 1)
            copy_x(s + 3, nc.scalar.copy)
            bias_on_scalar(s + 1)
            square(s)
            round_on_scalar(s)
            if s == 1:
                project(2)
            if s > 0:
                project(s + 2)
